import numpy as np
import ml_dtypes


def mxq(x, axis, fmt="e4m3"):
    dtype, down = {"e4m3": (ml_dtypes.float8_e4m3fn, 7), "e5m2": (ml_dtypes.float8_e5m2, 14)}[fmt]
    v = np.moveaxis(np.asarray(x, np.float32).astype(ml_dtypes.bfloat16).astype(np.float64), axis, -1)
    blocks = v.reshape(v.shape[:-1] + (-1, 32))
    amax = np.abs(blocks).max(-1, keepdims=True)
    byte = np.maximum(np.where(amax > 0, np.frexp(amax)[1] - 1 + 127, 0) - down, 1)
    scale = np.exp2(byte - 127.0)
    codes = (blocks / scale).astype(np.float32).astype(dtype).astype(np.float64)
    return np.moveaxis((codes * scale).reshape(v.shape), -1, axis)


WIDE = False


def mx_kscale(k):
    if not WIDE:
        return np.ones(k)
    levels = np.array([10, -10, 5, -5, 0])
    a = np.random.permutation(np.resize(levels, k // 512 * 4)).reshape(k // 512, 4)
    idx = np.arange(k)
    return np.exp2(a[idx // 512, idx % 128 // 32])


BF16 = ml_dtypes.bfloat16


def bf(x):
    return np.asarray(x, np.float32).astype(BF16)


def f64(x):
    return np.asarray(x).astype(np.float64)


B, IN, OUT, G, P = 512, 1024, 1024, 5, 3
NB = G + P
K = IN * NB
LO, HI = -1.0, 1.0
XE = 2.1875


def make_grid():
    gap = (HI - LO) / G
    g1d = np.arange(-P, G + P + 1) * gap + LO
    return np.broadcast_to(g1d, (IN, g1d.shape[0]))


def b_splines(x, grid):
    xg = x[:, :, None]
    bases = ((xg >= grid[:, :-1]) & (xg < grid[:, 1:])).astype(np.float64)
    for k in range(1, P + 1):
        left = (xg - grid[:, :-(k + 1)]) / (grid[:, k:-1] - grid[:, :-(k + 1)])
        right = (grid[:, k + 1:] - xg) / (grid[:, k + 1:] - grid[:, 1:-k])
        bases = left * bases[:, :, :-1] + right * bases[:, :, 1:]
    return bases


def setup_inputs():
    s = mx_kscale(K)
    edge = np.any(s != 1.0) & ((np.arange(IN) // (32 // NB)) % 2 == 1)
    x = np.random.standard_normal((B, IN))
    sign = np.where(np.random.standard_normal((B, IN)) < 0, -1.0, 1.0)
    x = np.where(edge[None, :], sign * XE, x)
    w = np.random.standard_normal((OUT, IN, NB)) * 3.2 / np.sqrt(IN)
    w = w * np.where(edge, 2.0 ** 18, 1.0)[None, :, None]
    return {"x": bf(x), "spline_weight": bf(w)}


def reference(x, spline_weight):
    grid = make_grid()
    bases = b_splines(f64(x), grid)
    bq = mxq(bases.reshape(B, K), 1, "e4m3")
    wq = mxq(f64(spline_weight).reshape(OUT, K), 1, "e4m3")
    return bq @ wq.T

@@ -1,0 +1,172 @@
+from contextlib import ExitStack
+
+import concourse.mybir as mybir
+from concourse.masks import make_identity
+
+F32 = mybir.dt.float32
+BF16 = mybir.dt.bfloat16
+U32 = mybir.dt.uint32
+U8 = mybir.dt.uint8
+FP8X4 = mybir.dt.float8_e4m3fn_x4
+ACT = mybir.ActivationFunctionType
+ALU = mybir.AluOpType
+
+P = 128
+B, IN, OUT, NB = 512, 1024, 1024, 8
+K = IN * NB
+PASSES = K // 512
+FLOPS = 2 * B * K * OUT
+
+
+def tile_kanlinearnores_v2_kernel(tc, x, spline_weight, out):
+    nc = tc.nc
+    w2d = spline_weight.rearrange("o i g -> o (i g)")
+    with ExitStack() as ctx:
+        keep = ctx.enter_context(tc.tile_pool(name="keep", bufs=1))
+        raw = ctx.enter_context(tc.tile_pool(name="raw", bufs=2))
+        wgp = ctx.enter_context(tc.tile_pool(name="wgp", bufs=4))
+        tmp = ctx.enter_context(tc.tile_pool(name="tmp", bufs=3))
+        sgp = ctx.enter_context(tc.tile_pool(name="sgp", bufs=3))
+        ostp = ctx.enter_context(tc.tile_pool(name="ostp", bufs=3))
+        psum = ctx.enter_context(tc.psum_pool(name="psum", bufs=8))
+
+        ident = keep.tile([P, P], F32)
+        wcodes = keep.tile([P, PASSES, OUT], U32, align_bytes=64)
+        wscales = keep.tile([P, PASSES, OUT], U8, align_bytes=64)
+        bcodes = keep.tile([P, PASSES, B], U32, align_bytes=64)
+        bscales = keep.tile([P, PASSES, B], U8, align_bytes=64)
+        xt = keep.tile([P, 4 * B * 2], BF16, align_bytes=64)
+
+        xr = raw.tile([P, K], BF16, tag="raw")
+        nc.sync.dma_start(
+            out=xr[:, 0 : 4 * IN].rearrange("p (t i) -> p t i", t=4),
+            in_=x.rearrange("(t p) i -> p t i", p=P),
+        )
+        make_identity(nc, ident[:])
+
+        xwords = xr[:, 0 : 4 * IN].bitcast(F32).rearrange("p (t q s) -> p t q s", t=4, s=4)
+        xt_words = xt[:].bitcast(F32)
+        for j in range(4):
+            bank = psum.tile([P, 512], F32, tag="bank")
+            for bt in range(4):
+                nc.tensor.transpose(
+                    out=bank[:, bt * P : (bt + 1) * P], in_=xwords[:, bt, :, j], identity=ident[:]
+                )
+            if j % 2 == 0:
+                nc.scalar.copy(out=xt_words[:, j * 512 : (j + 1) * 512], in_=bank[:])
+            else:
+                nc.vector.tensor_copy(out=xt_words[:, j * 512 : (j + 1) * 512], in_=bank[:])
+
+        def w_tile(t):
+            wr = raw.tile([P, K], BF16, tag="raw")
+            nc.sync.dma_start(out=wr[:], in_=w2d[t * P : (t + 1) * P, :])
+            words = wr[:].bitcast(F32).rearrange("p (q s) -> p q s", s=32)
+            cols = slice(t * P, (t + 1) * P)
+            for k in range(8):
+                bank = psum.tile([P, 512], F32, tag="bank")
+                for cc in range(2):
+                    c = 2 * k + cc
+                    for u in range(2):
+                        s = 4 * (2 * (c // 4) + u) + c % 4
+                        nc.tensor.transpose(
+                            out=bank[:, (2 * cc + u) * P : (2 * cc + u + 1) * P],
+                            in_=words[:, :, s],
+                            identity=ident[:],
+                        )
+                wg = wgp.tile([P, 1024], BF16, align_bytes=64)
+                nc.scalar.copy(
+                    out=wg[:].bitcast(F32).rearrange("p (c o u) -> p c o u", c=2, u=2),
+                    in_=bank[:].rearrange("p (c u o) -> p c o u", c=2, u=2),
+                )
+                for cc in range(2):
+                    c = 2 * k + cc
+                    nc.vector.quantize_mx(
+                        out=wcodes[:, c, cols].bitcast(FP8X4),
+                        scales=wscales[:, c, cols],
+                        in_=wg[:, cc * 512 : (cc + 1) * 512],
+                    )
+
+        def bases_chunk(j, rp, bh):
+            xs = xt[:, j * 1024 + bh * 512 : j * 1024 + (bh + 1) * 512]
+            t1 = tmp.tile([P, 2, 512], F32, tag="t1")
+            t2 = tmp.tile([P, 2, 512], F32, tag="t2")
+            t3 = tmp.tile([P, 2, 512], F32, tag="t3")
+            sg = sgp.tile([P, 2, 512], BF16, tag="sg")
+            sig = sgp.tile([P, 1024], BF16, tag="sig")
+            for e in range(2):
+                r = 2 * rp + e
+                nc.scalar.activation(out=t1[:, e, :], in_=xs, func=ACT.Abs, bias=1.5 - r, scale=2.5)
+                nc.vector.tensor_scalar(
+                    out=sg[:, e, :], in0=xs, scalar1=0.4 * r - 0.6, scalar2=0.5,
+                    op0=ALU.is_ge, op1=ALU.subtract,
+                )
+            nc.scalar.activation(out=t1[:], in_=t1[:], func=ACT.Abs, bias=-2.0, scale=1.0)
+            nc.scalar.activation(out=t2[:], in_=t1[:], func=ACT.Square)
+            nc.vector.tensor_scalar(
+                out=t1[:], in0=t1[:], scalar1=2.0, scalar2=2.0, op0=ALU.min, op1=ALU.subtract
+            )
+            nc.scalar.activation(out=t3[:], in_=t1[:], func=ACT.Square)
+            nc.vector.scalar_tensor_tensor(
+                out=t3[:], in0=t1[:], scalar=-1.0 / 6.0, in1=t3[:], op0=ALU.mult, op1=ALU.mult
+            )
+            nc.vector.scalar_tensor_tensor(
+                out=t2[:], in0=t1[:], scalar=0.5, in1=t2[:], op0=ALU.mult, op1=ALU.mult
+            )
+            nc.vector.scalar_tensor_tensor(
+                out=t2[:], in0=t2[:], scalar=2.0 / 3.0, in1=t3[:], op0=ALU.add, op1=ALU.min
+            )
+            nc.vector.tensor_tensor(
+                out=sig[:].rearrange("p (n e) -> p n e", e=2),
+                in0=t2[:].rearrange("p e n -> p n e"),
+                in1=sg[:].rearrange("p e n -> p n e"),
+                op=ALU.mult,
+            )
+            bcols = slice(bh * 256, (bh + 1) * 256)
+            for h in range(2):
+                c = 4 * j + rp + 2 * h
+                ob = sgp.tile([P, 1024], BF16, tag="ob", align_bytes=64)
+                nc.vector.tensor_scalar(
+                    out=ob[:], in0=sig[:], scalar1=(-2.0, 2.0)[h], scalar2=0.0,
+                    op0=ALU.mult, op1=ALU.max,
+                )
+                nc.vector.quantize_mx(
+                    out=bcodes[:, c, bcols].bitcast(FP8X4), scales=bscales[:, c, bcols], in_=ob[:]
+                )
+
+        chunks = [(j, rp, bh) for j in range(4) for rp in range(2) for bh in range(2)]
+
+        for t in range(8):
+            w_tile(t)
+            bases_chunk(*chunks[t])
+
+        acc = [[psum.tile([P, 512], F32, tag="bank", name="acc%d%d" % (m, n)) for n in range(2)] for m in range(4)]
+
+        def mx(j, rp, bh):
+            for h in range(2):
+                c = 4 * j + rp + 2 * h
+                for m in (2 * bh, 2 * bh + 1):
+                    for n in range(2):
+                        nc.tensor.matmul_mx(
+                            out=acc[m][n][:],
+                            lhsT=bcodes[:, c, m * P : (m + 1) * P].bitcast(FP8X4),
+                            lhsT_scale=bscales[:, c, m * P : (m + 1) * P],
+                            rhs=wcodes[:, c, n * 512 : (n + 1) * 512].bitcast(FP8X4),
+                            rhs_scale=wscales[:, c, n * 512 : (n + 1) * 512],
+                            start=(j == 0 and rp == 0 and h == 0),
+                            stop=(j == 3 and rp == 1 and h == 1),
+                        )
+
+        for ci in range(8):
+            mx(*chunks[ci])
+        for ci in range(8, 16):
+            bases_chunk(*chunks[ci])
+            mx(*chunks[ci])
+
+        for m in range(4):
+            for n in range(2):
+                ost = ostp.tile([P, 512], F32)
+                if n == 0:
+                    nc.scalar.copy(out=ost[:], in_=acc[m][n][:])
+                else:
+                    nc.vector.tensor_copy(out=ost[:], in_=acc[m][n][:])
+                nc.sync.dma_start(out=out[m * P : (m + 1) * P, n * 512 : (n + 1) * 512], in_=ost[:])

@@ -28,7 +28,8 @@ def tile_kanlinearnores_v2_kernel(tc, x, spline_weight, out):
         tmp = ctx.enter_context(tc.tile_pool(name="tmp", bufs=3))
         sgp = ctx.enter_context(tc.tile_pool(name="sgp", bufs=3))
         ostp = ctx.enter_context(tc.tile_pool(name="ostp", bufs=3))
-        psum = ctx.enter_context(tc.psum_pool(name="psum", bufs=8))
+        psum = ctx.enter_context(tc.psum_pool(name="psum", bufs=4))
+        accp = ctx.enter_context(tc.psum_pool(name="accp", bufs=1))
 
         ident = keep.tile([P, P], F32)
         wcodes = keep.tile([P, PASSES, OUT], U32, align_bytes=64)
@@ -38,10 +39,8 @@ def tile_kanlinearnores_v2_kernel(tc, x, spline_weight, out):
         xt = keep.tile([P, 4 * B * 2], BF16, align_bytes=64)
 
         xr = raw.tile([P, K], BF16, tag="raw")
-        nc.sync.dma_start(
-            out=xr[:, 0 : 4 * IN].rearrange("p (t i) -> p t i", t=4),
-            in_=x.rearrange("(t p) i -> p t i", p=P),
-        )
+        for bt in range(4):
+            nc.sync.dma_start(out=xr[:, bt * IN : (bt + 1) * IN], in_=x[bt * P : (bt + 1) * P, :])
         make_identity(nc, ident[:])
 
         xwords = xr[:, 0 : 4 * IN].bitcast(F32).rearrange("p (t q s) -> p t q s", t=4, s=4)
@@ -57,60 +56,75 @@ def tile_kanlinearnores_v2_kernel(tc, x, spline_weight, out):
             else:
                 nc.vector.tensor_copy(out=xt_words[:, j * 512 : (j + 1) * 512], in_=bank[:])
 
-        def w_tile(t):
-            wr = raw.tile([P, K], BF16, tag="raw")
-            nc.sync.dma_start(out=wr[:], in_=w2d[t * P : (t + 1) * P, :])
-            words = wr[:].bitcast(F32).rearrange("p (q s) -> p q s", s=32)
-            cols = slice(t * P, (t + 1) * P)
-            for k in range(8):
-                bank = psum.tile([P, 512], F32, tag="bank")
-                for cc in range(2):
-                    c = 2 * k + cc
-                    for u in range(2):
-                        s = 4 * (2 * (c // 4) + u) + c % 4
-                        nc.tensor.transpose(
-                            out=bank[:, (2 * cc + u) * P : (2 * cc + u + 1) * P],
-                            in_=words[:, :, s],
-                            identity=ident[:],
-                        )
-                wg = wgp.tile([P, 1024], BF16, align_bytes=64)
-                nc.scalar.copy(
-                    out=wg[:].bitcast(F32).rearrange("p (c o u) -> p c o u", c=2, u=2),
-                    in_=bank[:].rearrange("p (c u o) -> p c o u", c=2, u=2),
-                )
-                for cc in range(2):
-                    c = 2 * k + cc
-                    nc.vector.quantize_mx(
-                        out=wcodes[:, c, cols].bitcast(FP8X4),
-                        scales=wscales[:, c, cols],
-                        in_=wg[:, cc * 512 : (cc + 1) * 512],
-                    )
+        state = {}
 
-        def bases_chunk(j, rp, bh):
+        def w_unit(q):
+            t, k = divmod(q, 8)
+            if k == 0:
+                wr = raw.tile([P, K], BF16, tag="raw")
+                nc.sync.dma_start(out=wr[:], in_=w2d[t * P : (t + 1) * P, :])
+                state["words"] = wr[:].bitcast(F32).rearrange("p (q s) -> p q s", s=32)
+            words = state["words"]
+            cols = slice(t * P, (t + 1) * P)
+            bank = psum.tile([P, 512], F32, tag="bank")
+            for cc in range(2):
+                c = 2 * k + cc
+                for u in range(2):
+                    s = 4 * (2 * (c // 4) + u) + c % 4
+                    nc.tensor.transpose(
+                        out=bank[:, (2 * cc + u) * P : (2 * cc + u + 1) * P],
+                        in_=words[:, :, s],
+                        identity=ident[:],
+                    )
+            wg = wgp.tile([P, 1024], BF16, align_bytes=64)
+            nc.scalar.copy(
+                out=wg[:].bitcast(F32).rearrange("p (c o u) -> p c o u", c=2, u=2),
+                in_=bank[:].rearrange("p (c u o) -> p c o u", c=2, u=2),
+            )
+            for cc in range(2):
+                c = 2 * k + cc
+                nc.vector.quantize_mx(
+                    out=wcodes[:, c, cols].bitcast(FP8X4),
+                    scales=wscales[:, c, cols],
+                    in_=wg[:, cc * 512 : (cc + 1) * 512],
+                )
+
+        def signs(j, rp):
+            sg = sgp.tile([P, 2, 1024], BF16, tag="sg", bufs=2)
+            for e in range(2):
+                nc.vector.tensor_scalar(
+                    out=sg[:, e, :], in0=xt[:, j * 1024 : (j + 1) * 1024],
+                    scalar1=0.4 * (2 * rp + e) - 0.6, scalar2=0.5, op0=ALU.is_ge, op1=ALU.subtract,
+                )
+            return sg
+
+        def bases_chunk(ci, sg, relu_on_act):
+            j, rp, bh = chunks[ci]
             xs = xt[:, j * 1024 + bh * 512 : j * 1024 + (bh + 1) * 512]
             t1 = tmp.tile([P, 2, 512], F32, tag="t1")
             t2 = tmp.tile([P, 2, 512], F32, tag="t2")
             t3 = tmp.tile([P, 2, 512], F32, tag="t3")
-            sg = sgp.tile([P, 2, 512], BF16, tag="sg")
-            sig = sgp.tile([P, 1024], BF16, tag="sig")
+            sig = sgp.tile([P, 1024], BF16, tag="sig", bufs=2)
             for e in range(2):
-                r = 2 * rp + e
-                nc.scalar.activation(out=t1[:, e, :], in_=xs, func=ACT.Abs, bias=1.5 - r, scale=2.5)
-                nc.vector.tensor_scalar(
-                    out=sg[:, e, :], in0=xs, scalar1=0.4 * r - 0.6, scalar2=0.5,
-                    op0=ALU.is_ge, op1=ALU.subtract,
+                nc.scalar.activation(
+                    out=t1[:, e, :], in_=xs, func=ACT.Abs, bias=1.5 - (2 * rp + e), scale=2.5
                 )
             nc.scalar.activation(out=t1[:], in_=t1[:], func=ACT.Abs, bias=-2.0, scale=1.0)
             nc.scalar.activation(out=t2[:], in_=t1[:], func=ACT.Square)
-            nc.vector.tensor_scalar(
-                out=t1[:], in0=t1[:], scalar1=2.0, scalar2=2.0, op0=ALU.min, op1=ALU.subtract
-            )
+            if relu_on_act:
+                nc.scalar.activation(out=t1[:], in_=t1[:], func=ACT.Relu, bias=2.0, scale=-1.0)
+                sa = 1.0
+            else:
+                nc.vector.tensor_scalar(
+                    out=t1[:], in0=t1[:], scalar1=2.0, scalar2=2.0, op0=ALU.min, op1=ALU.subtract
+                )
+                sa = -1.0
             nc.scalar.activation(out=t3[:], in_=t1[:], func=ACT.Square)
             nc.vector.scalar_tensor_tensor(
-                out=t3[:], in0=t1[:], scalar=-1.0 / 6.0, in1=t3[:], op0=ALU.mult, op1=ALU.mult
+                out=t3[:], in0=t1[:], scalar=sa / 6.0, in1=t3[:], op0=ALU.mult, op1=ALU.mult
             )
             nc.vector.scalar_tensor_tensor(
-                out=t2[:], in0=t1[:], scalar=0.5, in1=t2[:], op0=ALU.mult, op1=ALU.mult
+                out=t2[:], in0=t1[:], scalar=-0.5 * sa, in1=t2[:], op0=ALU.mult, op1=ALU.mult
             )
             nc.vector.scalar_tensor_tensor(
                 out=t2[:], in0=t2[:], scalar=2.0 / 3.0, in1=t3[:], op0=ALU.add, op1=ALU.min
@@ -118,55 +132,67 @@ def tile_kanlinearnores_v2_kernel(tc, x, spline_weight, out):
             nc.vector.tensor_tensor(
                 out=sig[:].rearrange("p (n e) -> p n e", e=2),
                 in0=t2[:].rearrange("p e n -> p n e"),
-                in1=sg[:].rearrange("p e n -> p n e"),
+                in1=sg[:, :, bh * 512 : (bh + 1) * 512].rearrange("p e n -> p n e"),
                 op=ALU.mult,
             )
-            bcols = slice(bh * 256, (bh + 1) * 256)
+            ob = sgp.tile([P, 2, 1024], BF16, tag="ob", bufs=2, align_bytes=64)
             for h in range(2):
-                c = 4 * j + rp + 2 * h
-                ob = sgp.tile([P, 1024], BF16, tag="ob", align_bytes=64)
                 nc.vector.tensor_scalar(
-                    out=ob[:], in0=sig[:], scalar1=(-2.0, 2.0)[h], scalar2=0.0,
+                    out=ob[:, h, :], in0=sig[:], scalar1=(-2.0, 2.0)[h], scalar2=0.0,
                     op0=ALU.mult, op1=ALU.max,
                 )
-                nc.vector.quantize_mx(
-                    out=bcodes[:, c, bcols].bitcast(FP8X4), scales=bscales[:, c, bcols], in_=ob[:]
-                )
+            nc.vector.quantize_mx(
+                out=bcodes[:, ci, :].bitcast(FP8X4),
+                scales=bscales[:, ci, :],
+                in_=ob[:].rearrange("p h n -> p (h n)"),
+            )
 
         chunks = [(j, rp, bh) for j in range(4) for rp in range(2) for bh in range(2)]
+        acc = {}
 
-        for t in range(8):
-            w_tile(t)
-            bases_chunk(*chunks[t])
-
-        acc = [[psum.tile([P, 512], F32, tag="bank", name="acc%d%d" % (m, n)) for n in range(2)] for m in range(4)]
-
-        def mx(j, rp, bh):
+        def mx(ci, n):
+            j, rp, bh = chunks[ci]
             for h in range(2):
                 c = 4 * j + rp + 2 * h
                 for m in (2 * bh, 2 * bh + 1):
-                    for n in range(2):
-                        nc.tensor.matmul_mx(
-                            out=acc[m][n][:],
-                            lhsT=bcodes[:, c, m * P : (m + 1) * P].bitcast(FP8X4),
-                            lhsT_scale=bscales[:, c, m * P : (m + 1) * P],
-                            rhs=wcodes[:, c, n * 512 : (n + 1) * 512].bitcast(FP8X4),
-                            rhs_scale=wscales[:, c, n * 512 : (n + 1) * 512],
-                            start=(j == 0 and rp == 0 and h == 0),
-                            stop=(j == 3 and rp == 1 and h == 1),
-                        )
+                    nc.tensor.matmul_mx(
+                        out=acc[(m, n)][:],
+                        lhsT=bcodes[:, ci, h * 256 + (m % 2) * P : h * 256 + (m % 2 + 1) * P].bitcast(FP8X4),
+                        lhsT_scale=bscales[:, ci, h * 256 + (m % 2) * P : h * 256 + (m % 2 + 1) * P],
+                        rhs=wcodes[:, c, n * 512 : (n + 1) * 512].bitcast(FP8X4),
+                        rhs_scale=wscales[:, c, n * 512 : (n + 1) * 512],
+                        start=(j == 0 and rp == 0 and h == 0),
+                        stop=(j == 3 and rp == 1 and h == 1),
+                    )
 
-        for ci in range(8):
-            mx(*chunks[ci])
-        for ci in range(8, 16):
-            bases_chunk(*chunks[ci])
-            mx(*chunks[ci])
+        WSTEPS = 12
+        done_units = 0
+        for ci in range(16):
+            upto = min(64, (64 * (ci + 1) + WSTEPS - 1) // WSTEPS)
+            for q in range(done_units, upto):
+                w_unit(q)
+            before = done_units
+            done_units = upto
+            if chunks[ci][2] == 0:
+                state["sg"] = signs(chunks[ci][0], chunks[ci][1])
+            bases_chunk(ci, state["sg"], relu_on_act=(ci >= WSTEPS or ci % 2 == 1 and ci < 10))
+            for n in range(2):
+                need = 32 * (n + 1)
+                if done_units >= need:
+                    if before < need:
+                        for m in range(4):
+                            acc[(m, n)] = (accp if n == 0 else psum).tile(
+                                [P, 512], F32, tag=("acc%d" % m if n == 0 else "bank"), name="acc%d%d" % (m, n)
+                            )
+                        for cj in range(ci):
+                            mx(cj, n)
+                    mx(ci, n)
 
         for m in range(4):
             for n in range(2):
                 ost = ostp.tile([P, 512], F32)
-                if n == 0:
-                    nc.scalar.copy(out=ost[:], in_=acc[m][n][:])
+                if m < 2 or n == 0:
+                    nc.scalar.copy(out=ost[:], in_=acc[(m, n)][:])
                 else:
-                    nc.vector.tensor_copy(out=ost[:], in_=acc[m][n][:])
+                    nc.vector.tensor_copy(out=ost[:], in_=acc[(m, n)][:])
                 nc.sync.dma_start(out=out[m * P : (m + 1) * P, n * 512 : (n + 1) * 512], in_=ost[:])

@@ -17,6 +17,12 @@ K = IN * NB
 PASSES = K // 512
 FLOPS = 2 * B * K * OUT
 
+WSTEPS = 11
+RELU_ON_ACT_LAST = 4
+BANKS = 4
+MX_PER_W_STEP = 4
+MX_PER_STEP = 6
+
 
 def tile_kanlinearnores_v2_kernel(tc, x, spline_weight, out):
     nc = tc.nc
@@ -24,12 +30,12 @@ def tile_kanlinearnores_v2_kernel(tc, x, spline_weight, out):
     with ExitStack() as ctx:
         keep = ctx.enter_context(tc.tile_pool(name="keep", bufs=1))
         raw = ctx.enter_context(tc.tile_pool(name="raw", bufs=2))
-        wgp = ctx.enter_context(tc.tile_pool(name="wgp", bufs=4))
+        wgp = ctx.enter_context(tc.tile_pool(name="wgp", bufs=6))
         tmp = ctx.enter_context(tc.tile_pool(name="tmp", bufs=3))
-        sgp = ctx.enter_context(tc.tile_pool(name="sgp", bufs=3))
-        ostp = ctx.enter_context(tc.tile_pool(name="ostp", bufs=3))
-        psum = ctx.enter_context(tc.psum_pool(name="psum", bufs=4))
+        sgp = ctx.enter_context(tc.tile_pool(name="sgp", bufs=2))
+        psum = ctx.enter_context(tc.psum_pool(name="psum", bufs=BANKS))
         accp = ctx.enter_context(tc.psum_pool(name="accp", bufs=1))
+        ctx.enter_context(tc.manual_schedule())
 
         ident = keep.tile([P, P], F32)
         wcodes = keep.tile([P, PASSES, OUT], U32, align_bytes=64)
@@ -38,116 +44,179 @@ def tile_kanlinearnores_v2_kernel(tc, x, spline_weight, out):
         bscales = keep.tile([P, PASSES, B], U8, align_bytes=64)
         xt = keep.tile([P, 4 * B * 2], BF16, align_bytes=64)
 
+        make_identity(nc, ident[:])
         xr = raw.tile([P, K], BF16, tag="raw")
         for bt in range(4):
             nc.sync.dma_start(out=xr[:, bt * IN : (bt + 1) * IN], in_=x[bt * P : (bt + 1) * P, :])
-        make_identity(nc, ident[:])
-
-        xwords = xr[:, 0 : 4 * IN].bitcast(F32).rearrange("p (t q s) -> p t q s", t=4, s=4)
-        xt_words = xt[:].bitcast(F32)
-        for j in range(4):
-            bank = psum.tile([P, 512], F32, tag="bank")
-            for bt in range(4):
-                nc.tensor.transpose(
-                    out=bank[:, bt * P : (bt + 1) * P], in_=xwords[:, bt, :, j], identity=ident[:]
-                )
-            if j % 2 == 0:
-                nc.scalar.copy(out=xt_words[:, j * 512 : (j + 1) * 512], in_=bank[:])
-            else:
-                nc.vector.tensor_copy(out=xt_words[:, j * 512 : (j + 1) * 512], in_=bank[:])
 
         state = {}
+        banks = {}
+        staged = {}
 
-        def w_unit(q):
+        def w_load(t):
+            wr = raw.tile([P, K], BF16, tag="raw")
+            nc.sync.dma_start(out=wr[:], in_=w2d[t * P : (t + 1) * P, :])
+            state[t] = wr[:].bitcast(F32).rearrange("p (q s) -> p q s", s=32)
+
+        w_load(0)
+
+        xwords = xr[:, 0 : 4 * IN].bitcast(F32).rearrange("p (t q s) -> p t q s", t=4, s=4)
+        xt_jb = xt[:].bitcast(F32).rearrange("p (j b) -> p j b", j=4)
+        xbanks = [[psum.tile([P, 512], F32, tag="bank", name="xbank%d%d" % (jh, bh)) for bh in range(2)] for jh in range(2)]
+        for bt in range(4):
+            for j in range(4):
+                col = (j % 2) * 256 + (bt % 2) * P
+                nc.tensor.transpose(
+                    out=xbanks[j // 2][bt // 2][:, col : col + P], in_=xwords[:, bt, :, j], identity=ident[:]
+                )
+        for bh in range(2):
+            for jh in range(2):
+                dst = xt_jb[:, 2 * jh : 2 * jh + 2, bh * 256 : (bh + 1) * 256]
+                src = xbanks[jh][bh][:].rearrange("p (j b) -> p j b", j=2)
+                if (jh, bh) == (0, 0):
+                    nc.scalar.copy(out=dst, in_=src)
+                else:
+                    nc.vector.tensor_copy(out=dst, in_=src)
+        w_load(1)
+
+        def w_transposes(q):
+            if q >= 64:
+                return
             t, k = divmod(q, 8)
-            if k == 0:
-                wr = raw.tile([P, K], BF16, tag="raw")
-                nc.sync.dma_start(out=wr[:], in_=w2d[t * P : (t + 1) * P, :])
-                state["words"] = wr[:].bitcast(F32).rearrange("p (q s) -> p q s", s=32)
-            words = state["words"]
-            cols = slice(t * P, (t + 1) * P)
-            bank = psum.tile([P, 512], F32, tag="bank")
+            bank = psum.tile([P, 512], F32, tag="bank", name="wbank")
+            banks[q] = bank
             for cc in range(2):
                 c = 2 * k + cc
                 for u in range(2):
                     s = 4 * (2 * (c // 4) + u) + c % 4
                     nc.tensor.transpose(
                         out=bank[:, (2 * cc + u) * P : (2 * cc + u + 1) * P],
-                        in_=words[:, :, s],
+                        in_=state[t][:, :, s],
                         identity=ident[:],
                     )
-            wg = wgp.tile([P, 1024], BF16, align_bytes=64)
+            if k == 7 and t + 2 < 8:
+                w_load(t + 2)
+
+        def w_evac(q):
+            wg = wgp.tile([P, 1024], BF16, tag="wg", align_bytes=64)
+            staged[q] = wg
             nc.scalar.copy(
                 out=wg[:].bitcast(F32).rearrange("p (c o u) -> p c o u", c=2, u=2),
-                in_=bank[:].rearrange("p (c u o) -> p c o u", c=2, u=2),
+                in_=banks[q][:].rearrange("p (c u o) -> p c o u", c=2, u=2),
             )
+
+        def w_quant(q):
+            t, k = divmod(q, 8)
+            cols = slice(t * P, (t + 1) * P)
             for cc in range(2):
                 c = 2 * k + cc
                 nc.vector.quantize_mx(
                     out=wcodes[:, c, cols].bitcast(FP8X4),
                     scales=wscales[:, c, cols],
-                    in_=wg[:, cc * 512 : (cc + 1) * 512],
+                    in_=staged[q][:, cc * 512 : (cc + 1) * 512],
                 )
 
-        def signs(j, rp):
-            sg = sgp.tile([P, 2, 1024], BF16, tag="sg", bufs=2)
+        chunks = [(j, rp, bh) for j in range(4) for rp in range(2) for bh in range(2)]
+        n_chunks = len(chunks)
+        tl = {}
+
+        def on_act(ci):
+            return ci >= n_chunks - RELU_ON_ACT_LAST
+
+        def live(ci):
+            return 0 <= ci < n_chunks
+
+        def act_fold(ci, e):
+            j, rp, bh = chunks[ci]
+            if e == 0:
+                t1 = tmp.tile([P, 2, 512], F32, tag="t1", bufs=3)
+                tl[ci] = [t1, None, None]
+            nc.scalar.activation(
+                out=tl[ci][0][:, e, :], in_=xt[:, j * 1024 + bh * 512 : j * 1024 + (bh + 1) * 512],
+                func=ACT.Abs, bias=1.5 - (2 * rp + e), scale=2.5,
+            )
+
+        def act_dist(ci):
+            t1 = tl[ci][0]
+            nc.scalar.activation(out=t1[:], in_=t1[:], func=ACT.Abs, bias=-2.0, scale=1.0)
+
+        def act_vsq(ci):
+            t2 = tmp.tile([P, 2, 512], F32, tag="t2", bufs=4)
+            tl[ci][1] = t2
+            t1 = tl[ci][0]
+            nc.scalar.activation(out=t2[:], in_=t1[:], func=ACT.Square)
+            if on_act(ci):
+                nc.scalar.activation(out=t1[:], in_=t1[:], func=ACT.Relu, bias=2.0, scale=-1.0)
+
+        def dve_clamp(ci):
+            t1 = tl[ci][0]
+            nc.vector.tensor_scalar(
+                out=t1[:], in0=t1[:], scalar1=2.0, scalar2=2.0, op0=ALU.min, op1=ALU.subtract
+            )
+
+        def act_asq(ci):
+            t3 = tmp.tile([P, 2, 512], F32, tag="t3", bufs=3)
+            tl[ci][2] = t3
+            nc.scalar.activation(out=t3[:], in_=tl[ci][0][:], func=ACT.Square)
+
+        def sa(ci):
+            return 1.0 if on_act(ci) else -1.0
+
+        def dve_outer(ci):
+            t1, t2, t3 = tl[ci]
+            nc.vector.scalar_tensor_tensor(
+                out=t3[:], in0=t1[:], scalar=sa(ci) / 6.0, in1=t3[:], op0=ALU.mult, op1=ALU.mult
+            )
+
+        def dve_inner(ci):
+            t1, t2, t3 = tl[ci]
+            nc.vector.scalar_tensor_tensor(
+                out=t2[:], in0=t1[:], scalar=-0.5 * sa(ci), in1=t2[:], op0=ALU.mult, op1=ALU.mult
+            )
+
+        def dve_signs(ci):
+            j, rp, bh = chunks[ci]
+            sg = sgp.tile([P, 2, 1024], BF16, tag="sg")
+            state["sg"] = sg
             for e in range(2):
                 nc.vector.tensor_scalar(
                     out=sg[:, e, :], in0=xt[:, j * 1024 : (j + 1) * 1024],
                     scalar1=0.4 * (2 * rp + e) - 0.6, scalar2=0.5, op0=ALU.is_ge, op1=ALU.subtract,
                 )
-            return sg
 
-        def bases_chunk(ci, sg, relu_on_act):
-            j, rp, bh = chunks[ci]
-            xs = xt[:, j * 1024 + bh * 512 : j * 1024 + (bh + 1) * 512]
-            t1 = tmp.tile([P, 2, 512], F32, tag="t1")
-            t2 = tmp.tile([P, 2, 512], F32, tag="t2")
-            t3 = tmp.tile([P, 2, 512], F32, tag="t3")
-            sig = sgp.tile([P, 1024], BF16, tag="sig", bufs=2)
-            for e in range(2):
-                nc.scalar.activation(
-                    out=t1[:, e, :], in_=xs, func=ACT.Abs, bias=1.5 - (2 * rp + e), scale=2.5
-                )
-            nc.scalar.activation(out=t1[:], in_=t1[:], func=ACT.Abs, bias=-2.0, scale=1.0)
-            nc.scalar.activation(out=t2[:], in_=t1[:], func=ACT.Square)
-            if relu_on_act:
-                nc.scalar.activation(out=t1[:], in_=t1[:], func=ACT.Relu, bias=2.0, scale=-1.0)
-                sa = 1.0
-            else:
-                nc.vector.tensor_scalar(
-                    out=t1[:], in0=t1[:], scalar1=2.0, scalar2=2.0, op0=ALU.min, op1=ALU.subtract
-                )
-                sa = -1.0
-            nc.scalar.activation(out=t3[:], in_=t1[:], func=ACT.Square)
-            nc.vector.scalar_tensor_tensor(
-                out=t3[:], in0=t1[:], scalar=sa / 6.0, in1=t3[:], op0=ALU.mult, op1=ALU.mult
-            )
-            nc.vector.scalar_tensor_tensor(
-                out=t2[:], in0=t1[:], scalar=-0.5 * sa, in1=t2[:], op0=ALU.mult, op1=ALU.mult
-            )
+        def dve_min(ci):
+            t1, t2, t3 = tl[ci]
             nc.vector.scalar_tensor_tensor(
                 out=t2[:], in0=t2[:], scalar=2.0 / 3.0, in1=t3[:], op0=ALU.add, op1=ALU.min
             )
+
+        def dve_sign(ci):
+            bh = chunks[ci][2]
+            sig = sgp.tile([P, 1024], BF16, tag="sig")
+            tl[ci].append(sig)
             nc.vector.tensor_tensor(
                 out=sig[:].rearrange("p (n e) -> p n e", e=2),
-                in0=t2[:].rearrange("p e n -> p n e"),
-                in1=sg[:, :, bh * 512 : (bh + 1) * 512].rearrange("p e n -> p n e"),
+                in0=tl[ci][1][:].rearrange("p e n -> p n e"),
+                in1=state["sg"][:, :, bh * 512 : (bh + 1) * 512].rearrange("p e n -> p n e"),
                 op=ALU.mult,
             )
-            ob = sgp.tile([P, 2, 1024], BF16, tag="ob", bufs=2, align_bytes=64)
-            for h in range(2):
-                nc.vector.tensor_scalar(
-                    out=ob[:, h, :], in0=sig[:], scalar1=(-2.0, 2.0)[h], scalar2=0.0,
-                    op0=ALU.mult, op1=ALU.max,
-                )
+
+        def dve_split(ci, h):
+            if h == 0:
+                ob = sgp.tile([P, 2, 1024], BF16, tag="ob", align_bytes=64)
+                tl[ci].append(ob)
+            nc.vector.tensor_scalar(
+                out=tl[ci][4][:, h, :], in0=tl[ci][3][:], scalar1=(-2.0, 2.0)[h], scalar2=0.0,
+                op0=ALU.mult, op1=ALU.max,
+            )
+
+        def dve_quant(ci):
             nc.vector.quantize_mx(
                 out=bcodes[:, ci, :].bitcast(FP8X4),
                 scales=bscales[:, ci, :],
-                in_=ob[:].rearrange("p h n -> p (h n)"),
+                in_=tl[ci][4][:].rearrange("p h n -> p (h n)"),
             )
 
-        chunks = [(j, rp, bh) for j in range(4) for rp in range(2) for bh in range(2)]
         acc = {}
 
         def mx(ci, n):
@@ -155,43 +224,100 @@ def tile_kanlinearnores_v2_kernel(tc, x, spline_weight, out):
             for h in range(2):
                 c = 4 * j + rp + 2 * h
                 for m in (2 * bh, 2 * bh + 1):
+                    w0 = h * 256 + (m % 2) * P
                     nc.tensor.matmul_mx(
                         out=acc[(m, n)][:],
-                        lhsT=bcodes[:, ci, h * 256 + (m % 2) * P : h * 256 + (m % 2 + 1) * P].bitcast(FP8X4),
-                        lhsT_scale=bscales[:, ci, h * 256 + (m % 2) * P : h * 256 + (m % 2 + 1) * P],
+                        lhsT=bcodes[:, ci, w0 : w0 + P].bitcast(FP8X4),
+                        lhsT_scale=bscales[:, ci, w0 : w0 + P],
                         rhs=wcodes[:, c, n * 512 : (n + 1) * 512].bitcast(FP8X4),
                         rhs_scale=wscales[:, c, n * 512 : (n + 1) * 512],
                         start=(j == 0 and rp == 0 and h == 0),
                         stop=(j == 3 and rp == 1 and h == 1),
                     )
 
-        WSTEPS = 12
+        for q in range(BANKS):
+            w_transposes(q)
+
+        next_mx = [0, 0]
         done_units = 0
-        for ci in range(16):
-            upto = min(64, (64 * (ci + 1) + WSTEPS - 1) // WSTEPS)
-            for q in range(done_units, upto):
-                w_unit(q)
-            before = done_units
+        quantised = 0
+        for s in range(-3, n_chunks + 1):
+            upto = 0 if s < -1 else min(64, (64 * (s + 2) + WSTEPS - 1) // WSTEPS)
+            units = list(range(done_units, upto))
             done_units = upto
-            if chunks[ci][2] == 0:
-                state["sg"] = signs(chunks[ci][0], chunks[ci][1])
-            bases_chunk(ci, state["sg"], relu_on_act=(ci >= WSTEPS or ci % 2 == 1 and ci < 10))
+
+            act_list = []
+            if live(s + 3):
+                act_list.append((act_fold, (s + 3, 0)))
+                act_list.append((act_fold, (s + 3, 1)))
+            if live(s + 2):
+                act_list.append((act_asq, (s + 2,)))
+            if live(s + 3):
+                act_list.append((act_dist, (s + 3,)))
+                act_list.append((act_vsq, (s + 3,)))
+            if live(s + 2) and not on_act(s + 2):
+                dve_clamp(s + 2)
+            taken = 0
+            for i in range(-1, len(act_list)):
+                if i >= 0:
+                    act_list[i][0](*act_list[i][1])
+                if taken < len(units) and i != 0:
+                    w_evac(units[taken])
+                    w_transposes(units[taken] + BANKS)
+                    taken += 1
+            for q in units[taken:]:
+                w_evac(q)
+                w_transposes(q + BANKS)
+
+            dve_list = []
+            if live(s - 1):
+                dve_list.append((dve_quant, (s - 1,)))
+            if live(s) and chunks[s][2] == 0:
+                dve_list.append((dve_signs, (s,)))
+            if live(s):
+                dve_list.append((dve_min, (s,)))
+            if live(s + 1):
+                dve_list.append((dve_outer, (s + 1,)))
+            if live(s):
+                dve_list.append((dve_sign, (s,)))
+            if live(s + 1):
+                dve_list.append((dve_inner, (s + 1,)))
+            if live(s):
+                dve_list.append((dve_split, (s, 0)))
+                dve_list.append((dve_split, (s, 1)))
+            taken = 0
+            for i in range(len(dve_list)):
+                dve_list[i][0](*dve_list[i][1])
+                if taken < len(units) and i >= 1:
+                    w_quant(units[taken])
+                    taken += 1
+            for q in units[taken:]:
+                w_quant(q)
+            if live(s - 1):
+                quantised = s
+
+            budget = MX_PER_W_STEP if done_units < 64 else MX_PER_STEP
+            if s == n_chunks:
+                budget = 64
             for n in range(2):
-                need = 32 * (n + 1)
-                if done_units >= need:
-                    if before < need:
-                        for m in range(4):
-                            acc[(m, n)] = (accp if n == 0 else psum).tile(
-                                [P, 512], F32, tag=("acc%d" % m if n == 0 else "bank"), name="acc%d%d" % (m, n)
-                            )
-                        for cj in range(ci):
-                            mx(cj, n)
-                    mx(ci, n)
+                if done_units >= 32 * (n + 1) and (0, n) not in acc:
+                    for m in range(4):
+                        acc[(m, n)] = (accp if n == 0 else psum).tile(
+                            [P, 512], F32, tag=("acc%d" % m if n == 0 else "bank"), name="acc%d%d" % (m, n)
+                        )
+            while budget > 0:
+                cand = [n for n in range(2) if (0, n) in acc and next_mx[n] < quantised]
+                if not cand:
+                    break
+                n = min(cand, key=lambda v: next_mx[v])
+                mx(next_mx[n], n)
+                next_mx[n] += 1
+                budget -= 1
 
         for m in range(4):
             for n in range(2):
-                ost = ostp.tile([P, 512], F32)
-                if m < 2 or n == 0:
+                ost = wgp.tile([P, 512], F32, tag="wg", align_bytes=64)
+                if (m + n) % 2 == 0:
                     nc.scalar.copy(out=ost[:], in_=acc[(m, n)][:])
                 else:
                     nc.vector.tensor_copy(out=ost[:], in_=acc[(m, n)][:])

@@ -17,11 +17,9 @@ K = IN * NB
 PASSES = K // 512
 FLOPS = 2 * B * K * OUT
 
-WSTEPS = 11
+W_DONE_AT = 0.75
 RELU_ON_ACT_LAST = 4
-BANKS = 4
-MX_PER_W_STEP = 4
-MX_PER_STEP = 6
+OUT_ON_ACT_LAST = 2
 
 
 def tile_kanlinearnores_v2_kernel(tc, x, spline_weight, out):
@@ -30,38 +28,28 @@ def tile_kanlinearnores_v2_kernel(tc, x, spline_weight, out):
     with ExitStack() as ctx:
         keep = ctx.enter_context(tc.tile_pool(name="keep", bufs=1))
         raw = ctx.enter_context(tc.tile_pool(name="raw", bufs=2))
-        wgp = ctx.enter_context(tc.tile_pool(name="wgp", bufs=6))
-        tmp = ctx.enter_context(tc.tile_pool(name="tmp", bufs=3))
+        wgp = ctx.enter_context(tc.tile_pool(name="wgp", bufs=4))
+        tmp = ctx.enter_context(tc.tile_pool(name="tmp", bufs=4))
         sgp = ctx.enter_context(tc.tile_pool(name="sgp", bufs=2))
-        psum = ctx.enter_context(tc.psum_pool(name="psum", bufs=BANKS))
+        ostp = ctx.enter_context(tc.tile_pool(name="ostp", bufs=3))
+        psum = ctx.enter_context(tc.psum_pool(name="psum", bufs=4))
         accp = ctx.enter_context(tc.psum_pool(name="accp", bufs=1))
-        ctx.enter_context(tc.manual_schedule())
 
         ident = keep.tile([P, P], F32)
-        wcodes = keep.tile([P, PASSES, OUT], U32, align_bytes=64)
-        wscales = keep.tile([P, PASSES, OUT], U8, align_bytes=64)
-        bcodes = keep.tile([P, PASSES, B], U32, align_bytes=64)
-        bscales = keep.tile([P, PASSES, B], U8, align_bytes=64)
+        wcodes = keep.tile([P, 8, PASSES, P], U32, align_bytes=64)
+        wplanes = keep.tile([P, 2, PASSES, P], U8, align_bytes=64)
+        bcodes = keep.tile([P, PASSES * B], U32, align_bytes=64)
+        bscales = keep.tile([P, PASSES * B], U8, align_bytes=64)
         xt = keep.tile([P, 4 * B * 2], BF16, align_bytes=64)
 
-        make_identity(nc, ident[:])
         xr = raw.tile([P, K], BF16, tag="raw")
         for bt in range(4):
             nc.sync.dma_start(out=xr[:, bt * IN : (bt + 1) * IN], in_=x[bt * P : (bt + 1) * P, :])
-
-        state = {}
-        banks = {}
-        staged = {}
-
-        def w_load(t):
-            wr = raw.tile([P, K], BF16, tag="raw")
-            nc.sync.dma_start(out=wr[:], in_=w2d[t * P : (t + 1) * P, :])
-            state[t] = wr[:].bitcast(F32).rearrange("p (q s) -> p q s", s=32)
-
-        w_load(0)
+        make_identity(nc, ident[:])
 
         xwords = xr[:, 0 : 4 * IN].bitcast(F32).rearrange("p (t q s) -> p t q s", t=4, s=4)
-        xt_jb = xt[:].bitcast(F32).rearrange("p (j b) -> p j b", j=4)
+        xt_words = xt[:].bitcast(F32)
+        xt_jb = xt_words.rearrange("p (j b) -> p j b", j=4)
         xbanks = [[psum.tile([P, 512], F32, tag="bank", name="xbank%d%d" % (jh, bh)) for bh in range(2)] for jh in range(2)]
         for bt in range(4):
             for j in range(4):
@@ -73,251 +61,176 @@ def tile_kanlinearnores_v2_kernel(tc, x, spline_weight, out):
             for jh in range(2):
                 dst = xt_jb[:, 2 * jh : 2 * jh + 2, bh * 256 : (bh + 1) * 256]
                 src = xbanks[jh][bh][:].rearrange("p (j b) -> p j b", j=2)
-                if (jh, bh) == (0, 0):
+                if jh == 0:
                     nc.scalar.copy(out=dst, in_=src)
                 else:
                     nc.vector.tensor_copy(out=dst, in_=src)
-        w_load(1)
 
-        def w_transposes(q):
-            if q >= 64:
-                return
+        state = {}
+
+        def w_unit(q):
             t, k = divmod(q, 8)
-            bank = psum.tile([P, 512], F32, tag="bank", name="wbank")
-            banks[q] = bank
+            if k == 0:
+                wr = raw.tile([P, K], BF16, tag="raw")
+                nc.sync.dma_start(out=wr[:], in_=w2d[t * P : (t + 1) * P, :])
+                state["words"] = wr[:].bitcast(F32).rearrange("p (q s) -> p q s", s=32)
+            words = state["words"]
+            bank = psum.tile([P, 512], F32, tag="bank")
             for cc in range(2):
                 c = 2 * k + cc
                 for u in range(2):
                     s = 4 * (2 * (c // 4) + u) + c % 4
                     nc.tensor.transpose(
                         out=bank[:, (2 * cc + u) * P : (2 * cc + u + 1) * P],
-                        in_=state[t][:, :, s],
+                        in_=words[:, :, s],
                         identity=ident[:],
                     )
-            if k == 7 and t + 2 < 8:
-                w_load(t + 2)
-
-        def w_evac(q):
-            wg = wgp.tile([P, 1024], BF16, tag="wg", align_bytes=64)
-            staged[q] = wg
+            wg = wgp.tile([P, 1024], BF16, align_bytes=64)
             nc.scalar.copy(
                 out=wg[:].bitcast(F32).rearrange("p (c o u) -> p c o u", c=2, u=2),
-                in_=banks[q][:].rearrange("p (c u o) -> p c o u", c=2, u=2),
+                in_=bank[:].rearrange("p (c u o) -> p c o u", c=2, u=2),
+            )
+            nc.vector.quantize_mx(
+                out=wcodes[:, t, 2 * k : 2 * k + 2, :].rearrange("p c o -> p (c o)").bitcast(FP8X4),
+                scales=wplanes[4 * (t % 4) : P, t // 4, 2 * k : 2 * k + 2, :].rearrange("p c o -> p (c o)"),
+                in_=wg[:],
             )
 
-        def w_quant(q):
-            t, k = divmod(q, 8)
-            cols = slice(t * P, (t + 1) * P)
-            for cc in range(2):
-                c = 2 * k + cc
-                nc.vector.quantize_mx(
-                    out=wcodes[:, c, cols].bitcast(FP8X4),
-                    scales=wscales[:, c, cols],
-                    in_=staged[q][:, cc * 512 : (cc + 1) * 512],
-                )
-
-        chunks = [(j, rp, bh) for j in range(4) for rp in range(2) for bh in range(2)]
-        n_chunks = len(chunks)
-        tl = {}
-
-        def on_act(ci):
-            return ci >= n_chunks - RELU_ON_ACT_LAST
-
-        def live(ci):
-            return 0 <= ci < n_chunks
-
-        def act_fold(ci, e):
-            j, rp, bh = chunks[ci]
-            if e == 0:
-                t1 = tmp.tile([P, 2, 512], F32, tag="t1", bufs=3)
-                tl[ci] = [t1, None, None]
-            nc.scalar.activation(
-                out=tl[ci][0][:, e, :], in_=xt[:, j * 1024 + bh * 512 : j * 1024 + (bh + 1) * 512],
-                func=ACT.Abs, bias=1.5 - (2 * rp + e), scale=2.5,
-            )
-
-        def act_dist(ci):
-            t1 = tl[ci][0]
-            nc.scalar.activation(out=t1[:], in_=t1[:], func=ACT.Abs, bias=-2.0, scale=1.0)
-
-        def act_vsq(ci):
-            t2 = tmp.tile([P, 2, 512], F32, tag="t2", bufs=4)
-            tl[ci][1] = t2
-            t1 = tl[ci][0]
-            nc.scalar.activation(out=t2[:], in_=t1[:], func=ACT.Square)
-            if on_act(ci):
-                nc.scalar.activation(out=t1[:], in_=t1[:], func=ACT.Relu, bias=2.0, scale=-1.0)
-
-        def dve_clamp(ci):
-            t1 = tl[ci][0]
-            nc.vector.tensor_scalar(
-                out=t1[:], in0=t1[:], scalar1=2.0, scalar2=2.0, op0=ALU.min, op1=ALU.subtract
-            )
-
-        def act_asq(ci):
-            t3 = tmp.tile([P, 2, 512], F32, tag="t3", bufs=3)
-            tl[ci][2] = t3
-            nc.scalar.activation(out=t3[:], in_=tl[ci][0][:], func=ACT.Square)
-
-        def sa(ci):
-            return 1.0 if on_act(ci) else -1.0
-
-        def dve_outer(ci):
-            t1, t2, t3 = tl[ci]
-            nc.vector.scalar_tensor_tensor(
-                out=t3[:], in0=t1[:], scalar=sa(ci) / 6.0, in1=t3[:], op0=ALU.mult, op1=ALU.mult
-            )
-
-        def dve_inner(ci):
-            t1, t2, t3 = tl[ci]
-            nc.vector.scalar_tensor_tensor(
-                out=t2[:], in0=t1[:], scalar=-0.5 * sa(ci), in1=t2[:], op0=ALU.mult, op1=ALU.mult
-            )
-
-        def dve_signs(ci):
-            j, rp, bh = chunks[ci]
+        def signs(j, rp):
             sg = sgp.tile([P, 2, 1024], BF16, tag="sg")
-            state["sg"] = sg
             for e in range(2):
                 nc.vector.tensor_scalar(
                     out=sg[:, e, :], in0=xt[:, j * 1024 : (j + 1) * 1024],
                     scalar1=0.4 * (2 * rp + e) - 0.6, scalar2=0.5, op0=ALU.is_ge, op1=ALU.subtract,
                 )
+            return sg
 
-        def dve_min(ci):
-            t1, t2, t3 = tl[ci]
-            nc.vector.scalar_tensor_tensor(
-                out=t2[:], in0=t2[:], scalar=2.0 / 3.0, in1=t3[:], op0=ALU.add, op1=ALU.min
-            )
+        chunks = []
+        for j in range(4):
+            for rp in range(2):
+                sizes = (256, 256)
+                if (j, rp) == (0, 0):
+                    sizes = (128, 128, 256)
+                if (j, rp) == (3, 1):
+                    sizes = (256, 128, 128)
+                b0 = 0
+                for nb in sizes:
+                    chunks.append((j, rp, b0, nb, (4 * j + 2 * rp) * B + 2 * b0))
+                    b0 += nb
+        n_chunks = len(chunks)
 
-        def dve_sign(ci):
-            bh = chunks[ci][2]
+        def bases_chunk(ci, sg):
+            j, rp, b0, nb, off = chunks[ci]
+            n = 2 * nb
+            relu_on_act = ci >= n_chunks - RELU_ON_ACT_LAST
+            out_on_act = ci >= n_chunks - OUT_ON_ACT_LAST
+            xs = xt[:, j * 1024 + 2 * b0 : j * 1024 + 2 * b0 + n]
+            t1 = tmp.tile([P, 2, 512], F32, tag="t1")
+            t2 = tmp.tile([P, 2, 512], F32, tag="t2")
+            t3 = tmp.tile([P, 2, 512], F32, tag="t3")
             sig = sgp.tile([P, 1024], BF16, tag="sig")
-            tl[ci].append(sig)
+            a1, a2, a3 = t1[:, :, 0:n], t2[:, :, 0:n], t3[:, :, 0:n]
+            for e in range(2):
+                nc.scalar.activation(
+                    out=t1[:, e, 0:n], in_=xs, func=ACT.Abs, bias=1.5 - (2 * rp + e), scale=2.5
+                )
+            nc.scalar.activation(out=a1, in_=a1, func=ACT.Abs, bias=-2.0, scale=1.0)
+            nc.scalar.activation(out=a2, in_=a1, func=ACT.Square)
+            if relu_on_act:
+                nc.scalar.activation(out=a1, in_=a1, func=ACT.Relu, bias=2.0, scale=-1.0)
+                sa = 1.0
+            else:
+                nc.vector.tensor_scalar(
+                    out=a1, in0=a1, scalar1=2.0, scalar2=2.0, op0=ALU.min, op1=ALU.subtract
+                )
+                sa = -1.0
+            nc.scalar.activation(out=a3, in_=a1, func=ACT.Square)
+            nc.vector.scalar_tensor_tensor(
+                out=a3, in0=a1, scalar=sa / 6.0, in1=a3, op0=ALU.mult, op1=ALU.mult
+            )
+            nc.vector.scalar_tensor_tensor(
+                out=a2, in0=a1, scalar=-0.5 * sa, in1=a2, op0=ALU.mult, op1=ALU.mult
+            )
+            nc.vector.scalar_tensor_tensor(
+                out=a2, in0=a2, scalar=2.0 / 3.0, in1=a3, op0=ALU.add, op1=ALU.min
+            )
             nc.vector.tensor_tensor(
-                out=sig[:].rearrange("p (n e) -> p n e", e=2),
-                in0=tl[ci][1][:].rearrange("p e n -> p n e"),
-                in1=state["sg"][:, :, bh * 512 : (bh + 1) * 512].rearrange("p e n -> p n e"),
+                out=sig[:, 0 : 2 * n].rearrange("p (n e) -> p n e", e=2),
+                in0=a2.rearrange("p e n -> p n e"),
+                in1=sg[:, :, 2 * b0 : 2 * b0 + n].rearrange("p e n -> p n e"),
                 op=ALU.mult,
             )
-
-        def dve_split(ci, h):
-            if h == 0:
-                ob = sgp.tile([P, 2, 1024], BF16, tag="ob", align_bytes=64)
-                tl[ci].append(ob)
-            nc.vector.tensor_scalar(
-                out=tl[ci][4][:, h, :], in0=tl[ci][3][:], scalar1=(-2.0, 2.0)[h], scalar2=0.0,
-                op0=ALU.mult, op1=ALU.max,
-            )
-
-        def dve_quant(ci):
-            nc.vector.quantize_mx(
-                out=bcodes[:, ci, :].bitcast(FP8X4),
-                scales=bscales[:, ci, :],
-                in_=tl[ci][4][:].rearrange("p h n -> p (h n)"),
-            )
+            ob = sgp.tile([P, 2048], BF16, tag="ob", align_bytes=64)
+            split = ci == n_chunks - 1
+            for h in range(2):
+                oh = ob[:, h * 2 * n : (h + 1) * 2 * n]
+                if out_on_act:
+                    nc.scalar.activation(out=oh, in_=sig[:, 0 : 2 * n], func=ACT.Relu, scale=(-2.0, 2.0)[h])
+                else:
+                    nc.vector.tensor_scalar(
+                        out=oh, in0=sig[:, 0 : 2 * n], scalar1=(-2.0, 2.0)[h], scalar2=0.0,
+                        op0=ALU.mult, op1=ALU.max,
+                    )
+                if split:
+                    nc.vector.quantize_mx(
+                        out=bcodes[:, off + h * nb : off + (h + 1) * nb].bitcast(FP8X4),
+                        scales=bscales[:, off + h * nb : off + (h + 1) * nb],
+                        in_=oh,
+                    )
+            if not split:
+                nc.vector.quantize_mx(
+                    out=bcodes[:, off : off + 2 * nb].bitcast(FP8X4),
+                    scales=bscales[:, off : off + 2 * nb],
+                    in_=ob[:, 0 : 4 * n],
+                )
 
         acc = {}
 
         def mx(ci, n):
-            j, rp, bh = chunks[ci]
+            j, rp, b0, nb, off = chunks[ci]
             for h in range(2):
                 c = 4 * j + rp + 2 * h
-                for m in (2 * bh, 2 * bh + 1):
-                    w0 = h * 256 + (m % 2) * P
-                    nc.tensor.matmul_mx(
-                        out=acc[(m, n)][:],
-                        lhsT=bcodes[:, ci, w0 : w0 + P].bitcast(FP8X4),
-                        lhsT_scale=bscales[:, ci, w0 : w0 + P],
-                        rhs=wcodes[:, c, n * 512 : (n + 1) * 512].bitcast(FP8X4),
-                        rhs_scale=wscales[:, c, n * 512 : (n + 1) * 512],
-                        start=(j == 0 and rp == 0 and h == 0),
-                        stop=(j == 3 and rp == 1 and h == 1),
-                    )
-
-        for q in range(BANKS):
-            w_transposes(q)
-
-        next_mx = [0, 0]
-        done_units = 0
-        quantised = 0
-        for s in range(-3, n_chunks + 1):
-            upto = 0 if s < -1 else min(64, (64 * (s + 2) + WSTEPS - 1) // WSTEPS)
-            units = list(range(done_units, upto))
-            done_units = upto
-
-            act_list = []
-            if live(s + 3):
-                act_list.append((act_fold, (s + 3, 0)))
-                act_list.append((act_fold, (s + 3, 1)))
-            if live(s + 2):
-                act_list.append((act_asq, (s + 2,)))
-            if live(s + 3):
-                act_list.append((act_dist, (s + 3,)))
-                act_list.append((act_vsq, (s + 3,)))
-            if live(s + 2) and not on_act(s + 2):
-                dve_clamp(s + 2)
-            taken = 0
-            for i in range(-1, len(act_list)):
-                if i >= 0:
-                    act_list[i][0](*act_list[i][1])
-                if taken < len(units) and i != 0:
-                    w_evac(units[taken])
-                    w_transposes(units[taken] + BANKS)
-                    taken += 1
-            for q in units[taken:]:
-                w_evac(q)
-                w_transposes(q + BANKS)
-
-            dve_list = []
-            if live(s - 1):
-                dve_list.append((dve_quant, (s - 1,)))
-            if live(s) and chunks[s][2] == 0:
-                dve_list.append((dve_signs, (s,)))
-            if live(s):
-                dve_list.append((dve_min, (s,)))
-            if live(s + 1):
-                dve_list.append((dve_outer, (s + 1,)))
-            if live(s):
-                dve_list.append((dve_sign, (s,)))
-            if live(s + 1):
-                dve_list.append((dve_inner, (s + 1,)))
-            if live(s):
-                dve_list.append((dve_split, (s, 0)))
-                dve_list.append((dve_split, (s, 1)))
-            taken = 0
-            for i in range(len(dve_list)):
-                dve_list[i][0](*dve_list[i][1])
-                if taken < len(units) and i >= 1:
-                    w_quant(units[taken])
-                    taken += 1
-            for q in units[taken:]:
-                w_quant(q)
-            if live(s - 1):
-                quantised = s
-
-            budget = MX_PER_W_STEP if done_units < 64 else MX_PER_STEP
-            if s == n_chunks:
-                budget = 64
-            for n in range(2):
-                if done_units >= 32 * (n + 1) and (0, n) not in acc:
-                    for m in range(4):
-                        acc[(m, n)] = (accp if n == 0 else psum).tile(
-                            [P, 512], F32, tag=("acc%d" % m if n == 0 else "bank"), name="acc%d%d" % (m, n)
+                for mi in range(nb // P):
+                    w0 = off + h * nb + mi * P
+                    for tq in range(4):
+                        nc.tensor.matmul_mx(
+                            out=acc[(b0 // P + mi, n)][:, tq * P : (tq + 1) * P],
+                            lhsT=bcodes[:, w0 : w0 + P].bitcast(FP8X4),
+                            lhsT_scale=bscales[:, w0 : w0 + P],
+                            rhs=wcodes[:, 4 * n + tq, c, :].bitcast(FP8X4),
+                            rhs_scale=wplanes[4 * tq : P, n, c, :],
+                            start=(j == 0 and rp == 0 and h == 0 and tq == 0),
+                            stop=(j == 3 and rp == 1 and h == 1 and tq == 3),
                         )
-            while budget > 0:
-                cand = [n for n in range(2) if (0, n) in acc and next_mx[n] < quantised]
-                if not cand:
-                    break
-                n = min(cand, key=lambda v: next_mx[v])
-                mx(next_mx[n], n)
-                next_mx[n] += 1
-                budget -= 1
+
+        done_units = 0
+        done_b = 0
+        for ci in range(n_chunks):
+            done_b += chunks[ci][3]
+            upto = min(64, int(64 * done_b / (W_DONE_AT * 16 * 256) + 0.999))
+            for q in range(done_units, upto):
+                w_unit(q)
+            before = done_units
+            done_units = upto
+            if chunks[ci][2] == 0:
+                state["sg"] = signs(chunks[ci][0], chunks[ci][1])
+            bases_chunk(ci, state["sg"])
+            for n in range(2):
+                need = 32 * (n + 1)
+                if done_units >= need:
+                    if before < need:
+                        for m in range(4):
+                            acc[(m, n)] = (accp if n == 0 else psum).tile(
+                                [P, 512], F32, tag=("acc%d" % m if n == 0 else "bank"), name="acc%d%d" % (m, n)
+                            )
+                        for cj in range(ci):
+                            mx(cj, n)
+                    mx(ci, n)
 
         for m in range(4):
             for n in range(2):
-                ost = wgp.tile([P, 512], F32, tag="wg", align_bytes=64)
-                if (m + n) % 2 == 0:
+                ost = ostp.tile([P, 512], F32)
+                if m < 3 or n == 0:
                     nc.scalar.copy(out=ost[:], in_=acc[(m, n)][:])
                 else:
                     nc.vector.tensor_copy(out=ost[:], in_=acc[(m, n)][:])

@@ -18,6 +18,7 @@ PASSES = K // 512
 FLOPS = 2 * B * K * OUT
 
 W_DONE_AT = 0.75
+EVAC_ON_DVE_EVERY = 8
 RELU_ON_ACT_LAST = 4
 OUT_ON_ACT_LAST = 2
 
@@ -86,7 +87,7 @@ def tile_kanlinearnores_v2_kernel(tc, x, spline_weight, out):
                         identity=ident[:],
                     )
             wg = wgp.tile([P, 1024], BF16, align_bytes=64)
-            nc.scalar.copy(
+            (nc.vector.tensor_copy if q % EVAC_ON_DVE_EVERY == EVAC_ON_DVE_EVERY - 1 else nc.scalar.copy)(
                 out=wg[:].bitcast(F32).rearrange("p (c o u) -> p c o u", c=2, u=2),
                 in_=bank[:].rearrange("p (c u o) -> p c o u", c=2, u=2),
             )

@@ -18,9 +18,8 @@ PASSES = K // 512
 FLOPS = 2 * B * K * OUT
 
 W_DONE_AT = 0.75
-EVAC_ON_DVE_EVERY = 8
-RELU_ON_ACT_LAST = 4
-OUT_ON_ACT_LAST = 2
+RELU_ON_ACT_LAST = 18
+OUT_ON_ACT_LAST = 0
 
 
 def tile_kanlinearnores_v2_kernel(tc, x, spline_weight, out):
@@ -87,7 +86,7 @@ def tile_kanlinearnores_v2_kernel(tc, x, spline_weight, out):
                         identity=ident[:],
                     )
             wg = wgp.tile([P, 1024], BF16, align_bytes=64)
-            (nc.vector.tensor_copy if q % EVAC_ON_DVE_EVERY == EVAC_ON_DVE_EVERY - 1 else nc.scalar.copy)(
+            nc.scalar.copy(
                 out=wg[:].bitcast(F32).rearrange("p (c o u) -> p c o u", c=2, u=2),
                 in_=bank[:].rearrange("p (c u o) -> p c o u", c=2, u=2),
             )

@@ -18,8 +18,8 @@ PASSES = K // 512
 FLOPS = 2 * B * K * OUT
 
 W_DONE_AT = 0.75
-RELU_ON_ACT_LAST = 18
-OUT_ON_ACT_LAST = 0
+RELU_ON_ACT_LAST = 4
+OUT_ON_ACT_LAST = 2
 
 
 def tile_kanlinearnores_v2_kernel(tc, x, spline_weight, out):
@@ -122,7 +122,7 @@ def tile_kanlinearnores_v2_kernel(tc, x, spline_weight, out):
         def bases_chunk(ci, sg):
             j, rp, b0, nb, off = chunks[ci]
             n = 2 * nb
-            relu_on_act = ci >= n_chunks - RELU_ON_ACT_LAST
+            relu_on_act = ci >= n_chunks - RELU_ON_ACT_LAST or ci in (4, 7, 10, 13)
             out_on_act = ci >= n_chunks - OUT_ON_ACT_LAST
             xs = xt[:, j * 1024 + 2 * b0 : j * 1024 + 2 * b0 + n]
             t1 = tmp.tile([P, 2, 512], F32, tag="t1")

@@ -17,9 +17,12 @@ K = IN * NB
 PASSES = K // 512
 FLOPS = 2 * B * K * OUT
 
-W_DONE_AT = 0.75
-RELU_ON_ACT_LAST = 4
-OUT_ON_ACT_LAST = 2
+SLOTS = 12
+AHEAD_T = 3
+AHEAD_G = 2
+MX_SLOT = 2
+MX_LATE = 8
+R6 = 6.0 ** -0.5
 
 
 def tile_kanlinearnores_v2_kernel(tc, x, spline_weight, out):
@@ -29,9 +32,10 @@ def tile_kanlinearnores_v2_kernel(tc, x, spline_weight, out):
         keep = ctx.enter_context(tc.tile_pool(name="keep", bufs=1))
         raw = ctx.enter_context(tc.tile_pool(name="raw", bufs=2))
         wgp = ctx.enter_context(tc.tile_pool(name="wgp", bufs=4))
-        tmp = ctx.enter_context(tc.tile_pool(name="tmp", bufs=4))
-        sgp = ctx.enter_context(tc.tile_pool(name="sgp", bufs=2))
-        ostp = ctx.enter_context(tc.tile_pool(name="ostp", bufs=3))
+        tmp = ctx.enter_context(tc.tile_pool(name="tmp", bufs=2))
+        sgp = ctx.enter_context(tc.tile_pool(name="sgp", bufs=1))
+        utp = ctx.enter_context(tc.tile_pool(name="utp", bufs=1))
+        sg2 = ctx.enter_context(tc.tile_pool(name="sg2", bufs=2))
         psum = ctx.enter_context(tc.psum_pool(name="psum", bufs=4))
         accp = ctx.enter_context(tc.psum_pool(name="accp", bufs=1))
 
@@ -67,8 +71,9 @@ def tile_kanlinearnores_v2_kernel(tc, x, spline_weight, out):
                     nc.vector.tensor_copy(out=dst, in_=src)
 
         state = {}
+        banks, gathers = {}, {}
 
-        def w_unit(q):
+        def w_transpose(q):
             t, k = divmod(q, 8)
             if k == 0:
                 wr = raw.tile([P, K], BF16, tag="raw")
@@ -85,153 +90,267 @@ def tile_kanlinearnores_v2_kernel(tc, x, spline_weight, out):
                         in_=words[:, :, s],
                         identity=ident[:],
                     )
+            banks[q] = bank
+
+        def w_gather(q):
+            bank = banks.pop(q)
             wg = wgp.tile([P, 1024], BF16, align_bytes=64)
             nc.scalar.copy(
                 out=wg[:].bitcast(F32).rearrange("p (c o u) -> p c o u", c=2, u=2),
                 in_=bank[:].rearrange("p (c u o) -> p c o u", c=2, u=2),
             )
+            gathers[q] = wg
+
+        def w_quantise(q):
+            t, k = divmod(q, 8)
+            wg = gathers.pop(q)
             nc.vector.quantize_mx(
                 out=wcodes[:, t, 2 * k : 2 * k + 2, :].rearrange("p c o -> p (c o)").bitcast(FP8X4),
                 scales=wplanes[4 * (t % 4) : P, t // 4, 2 * k : 2 * k + 2, :].rearrange("p c o -> p (c o)"),
                 in_=wg[:],
             )
 
-        def signs(j, rp):
-            sg = sgp.tile([P, 2, 1024], BF16, tag="sg")
-            for e in range(2):
-                nc.vector.tensor_scalar(
-                    out=sg[:, e, :], in0=xt[:, j * 1024 : (j + 1) * 1024],
-                    scalar1=0.4 * (2 * rp + e) - 0.6, scalar2=0.5, op0=ALU.is_ge, op1=ALU.subtract,
-                )
-            return sg
-
         chunks = []
         for j in range(4):
-            for rp in range(2):
-                sizes = (256, 256)
-                if (j, rp) == (0, 0):
-                    sizes = (128, 128, 256)
-                if (j, rp) == (3, 1):
-                    sizes = (256, 128, 128)
-                b0 = 0
-                for nb in sizes:
-                    chunks.append((j, rp, b0, nb, (4 * j + 2 * rp) * B + 2 * b0))
-                    b0 += nb
+            sizes = {0: (128, 128, 256), 3: (256, 128, 128)}.get(j, (256, 256))
+            b0 = 0
+            for nb in sizes:
+                chunks.append((j, b0, nb, 4 * (j * B + b0)))
+                b0 += nb
         n_chunks = len(chunks)
 
-        def bases_chunk(ci, sg):
-            j, rp, b0, nb, off = chunks[ci]
+        def signs(j):
+            xs = xt[:, j * 1024 : (j + 1) * 1024]
+            yt = sgp.tile([P, 1024, 2], BF16, tag="yt")
+            sgt = sg2.tile([P, 2, 2048], BF16, tag="sgt")
+            y = yt[:].rearrange("p n e -> p (n e)")
+            return sgt, [
+                lambda: nc.vector.tensor_copy(out=yt[:, :, 0], in_=xs),
+                lambda: nc.vector.tensor_scalar_add(out=yt[:, :, 1], in0=xs, scalar1=-0.4),
+                lambda: nc.vector.tensor_scalar(
+                    out=sgt[:, 0, :], in0=y, scalar1=-0.6, scalar2=0.5, op0=ALU.is_ge, op1=ALU.subtract
+                ),
+                lambda: nc.vector.tensor_scalar(
+                    out=sgt[:, 1, :], in0=y, scalar1=0.2, scalar2=1.0, op0=ALU.is_ge, op1=ALU.mult
+                ),
+                lambda: nc.vector.tensor_scalar(
+                    out=y, in0=y, scalar1=-1.402, scalar2=-0.5, op0=ALU.is_ge, op1=ALU.mult
+                ),
+                lambda: nc.vector.tensor_tensor(out=sgt[:, 1, :], in0=sgt[:, 1, :], in1=y, op=ALU.add),
+            ]
+
+        def distances(ci):
+            j, b0, nb, off = chunks[ci]
             n = 2 * nb
-            relu_on_act = ci >= n_chunks - RELU_ON_ACT_LAST or ci in (4, 7, 10, 13)
-            out_on_act = ci >= n_chunks - OUT_ON_ACT_LAST
             xs = xt[:, j * 1024 + 2 * b0 : j * 1024 + 2 * b0 + n]
-            t1 = tmp.tile([P, 2, 512], F32, tag="t1")
-            t2 = tmp.tile([P, 2, 512], F32, tag="t2")
-            t3 = tmp.tile([P, 2, 512], F32, tag="t3")
-            sig = sgp.tile([P, 1024], BF16, tag="sig")
-            a1, a2, a3 = t1[:, :, 0:n], t2[:, :, 0:n], t3[:, :, 0:n]
-            for e in range(2):
+            td = tmp.tile([P, 2, 512], F32, tag="td")
+            td2 = tmp.tile([P, 2, 512], F32, tag="td2")
+            ta = tmp.tile([P, 2, 512], F32, tag="ta")
+            tb = tmp.tile([P, 2, 512], F32, tag="tb")
+            th = tmp.tile([P, 2, 512], F32, tag="th")
+            tw = tmp.tile([P, 2, 512], F32, tag="tw")
+            d0, d2, sa, sb, h, w2 = (t[:, :, 0:n] for t in (td, td2, ta, tb, th, tw))
+            state[ci] = (d0, d2, sa, sb, h, w2)
+
+            def first():
+                for e in range(2):
+                    nc.scalar.activation(out=td[:, e, 0:n], in_=xs, func=ACT.Abs, bias=1.5 - e, scale=2.5)
+
+            return [
+                first,
+                lambda: nc.scalar.activation(out=d0, in_=d0, func=ACT.Abs, bias=-2.0, scale=1.0),
+                lambda: nc.scalar.activation(out=d2, in_=d0, func=ACT.Abs, bias=-2.0, scale=1.0),
+                lambda: nc.scalar.activation(out=h, in_=d2, func=ACT.Abs, bias=-1.0, scale=1.0),
+                lambda: nc.scalar.activation(out=w2, in_=h, func=ACT.Square, bias=1.0, scale=-1.0),
+                lambda: nc.scalar.activation(out=sa, in_=d2, func=ACT.Square, scale=R6),
+                lambda: nc.scalar.activation(out=sb, in_=d2, func=ACT.Square, bias=2.0 * R6, scale=-R6),
+            ]
+
+        def values(ci, sgt):
+            j, b0, nb, off = chunks[ci]
+            n = 2 * nb
+            d0, d2, sa, sb, h, w2 = state.pop(ci)
+            ngt = sgp.tile([P, 1024], BF16, tag="ng")
+            ut = utp.tile([P, 2, 1024], BF16, tag="ut")
+            ob = sgp.tile([P, 4096], BF16, tag="ob", align_bytes=64)
+            ng = ngt[:, 0 : 2 * n]
+            u = [ut[:, r, 0 : 2 * n] for r in range(2)]
+            both = ut[:, :, 0 : 2 * n]
+            humps = ob[:, 0 : 8 * n].rearrange("p (r h n) -> p r h n", r=2, h=2)
+
+            def inner_cubic():
+                nc.vector.scalar_tensor_tensor(out=w2, in0=h, scalar=1.0, in1=w2, op0=ALU.add, op1=ALU.mult)
+
+            def inner():
                 nc.scalar.activation(
-                    out=t1[:, e, 0:n], in_=xs, func=ACT.Abs, bias=1.5 - (2 * rp + e), scale=2.5
+                    out=ng.rearrange("p (n e) -> p n e", e=2), in_=w2.rearrange("p e n -> p n e"),
+                    func=ACT.Identity, bias=-2.0 / 3.0, scale=0.5,
                 )
-            nc.scalar.activation(out=a1, in_=a1, func=ACT.Abs, bias=-2.0, scale=1.0)
-            nc.scalar.activation(out=a2, in_=a1, func=ACT.Square)
-            if relu_on_act:
-                nc.scalar.activation(out=a1, in_=a1, func=ACT.Relu, bias=2.0, scale=-1.0)
-                sa = 1.0
-            else:
+
+            def outer(r):
+                dist, sq = ((d0, sa), (d2, sb))[r]
+                nc.vector.scalar_tensor_tensor(
+                    out=u[r].rearrange("p (n e) -> p n e", e=2), in0=dist.rearrange("p e n -> p n e"), scalar=2.0,
+                    in1=sq.rearrange("p e n -> p n e"), op0=ALU.subtract, op1=ALU.mult,
+                )
+
+            def join(r):
+                nc.vector.tensor_tensor(out=u[r], in0=u[r], in1=ng, op=ALU.max)
+
+            def clamp():
+                nc.vector.tensor_scalar_min(out=both, in0=both, scalar1=0.0)
+
+            def sign():
+                nc.vector.tensor_tensor(out=both, in0=both, in1=sgt[:, :, 4 * b0 : 4 * (b0 + nb)], op=ALU.mult)
+
+            def split(hh):
                 nc.vector.tensor_scalar(
-                    out=a1, in0=a1, scalar1=2.0, scalar2=2.0, op0=ALU.min, op1=ALU.subtract
+                    out=humps[:, :, hh, :], in0=both, scalar1=(2.0, -2.0)[hh], scalar2=0.0, op0=ALU.mult, op1=ALU.max
                 )
-                sa = -1.0
-            nc.scalar.activation(out=a3, in_=a1, func=ACT.Square)
-            nc.vector.scalar_tensor_tensor(
-                out=a3, in0=a1, scalar=sa / 6.0, in1=a3, op0=ALU.mult, op1=ALU.mult
-            )
-            nc.vector.scalar_tensor_tensor(
-                out=a2, in0=a1, scalar=-0.5 * sa, in1=a2, op0=ALU.mult, op1=ALU.mult
-            )
-            nc.vector.scalar_tensor_tensor(
-                out=a2, in0=a2, scalar=2.0 / 3.0, in1=a3, op0=ALU.add, op1=ALU.min
-            )
-            nc.vector.tensor_tensor(
-                out=sig[:, 0 : 2 * n].rearrange("p (n e) -> p n e", e=2),
-                in0=a2.rearrange("p e n -> p n e"),
-                in1=sg[:, :, 2 * b0 : 2 * b0 + n].rearrange("p e n -> p n e"),
-                op=ALU.mult,
-            )
-            ob = sgp.tile([P, 2048], BF16, tag="ob", align_bytes=64)
-            split = ci == n_chunks - 1
-            for h in range(2):
-                oh = ob[:, h * 2 * n : (h + 1) * 2 * n]
-                if out_on_act:
-                    nc.scalar.activation(out=oh, in_=sig[:, 0 : 2 * n], func=ACT.Relu, scale=(-2.0, 2.0)[h])
-                else:
-                    nc.vector.tensor_scalar(
-                        out=oh, in0=sig[:, 0 : 2 * n], scalar1=(-2.0, 2.0)[h], scalar2=0.0,
-                        op0=ALU.mult, op1=ALU.max,
-                    )
-                if split:
-                    nc.vector.quantize_mx(
-                        out=bcodes[:, off + h * nb : off + (h + 1) * nb].bitcast(FP8X4),
-                        scales=bscales[:, off + h * nb : off + (h + 1) * nb],
-                        in_=oh,
-                    )
-            if not split:
+
+            def quantise(r):
+                w0 = off + r * 2 * nb
                 nc.vector.quantize_mx(
-                    out=bcodes[:, off : off + 2 * nb].bitcast(FP8X4),
-                    scales=bscales[:, off : off + 2 * nb],
-                    in_=ob[:, 0 : 4 * n],
+                    out=bcodes[:, w0 : w0 + 2 * nb].bitcast(FP8X4),
+                    scales=bscales[:, w0 : w0 + 2 * nb],
+                    in_=ob[:, r * 4 * n : (r + 1) * 4 * n],
                 )
+
+            return inner_cubic, inner, outer, join, clamp, sign, split, quantise
 
         acc = {}
+        groups = {0: [], 1: []}
+        opened = {0: False, 1: False}
 
-        def mx(ci, n):
-            j, rp, b0, nb, off = chunks[ci]
-            for h in range(2):
-                c = 4 * j + rp + 2 * h
-                for mi in range(nb // P):
-                    w0 = off + h * nb + mi * P
-                    for tq in range(4):
-                        nc.tensor.matmul_mx(
-                            out=acc[(b0 // P + mi, n)][:, tq * P : (tq + 1) * P],
-                            lhsT=bcodes[:, w0 : w0 + P].bitcast(FP8X4),
-                            lhsT_scale=bscales[:, w0 : w0 + P],
-                            rhs=wcodes[:, 4 * n + tq, c, :].bitcast(FP8X4),
-                            rhs_scale=wplanes[4 * tq : P, n, c, :],
-                            start=(j == 0 and rp == 0 and h == 0 and tq == 0),
-                            stop=(j == 3 and rp == 1 and h == 1 and tq == 3),
-                        )
+        def mx_group(n, ci, q, mi):
+            j, b0, nb, off = chunks[ci]
+            c = 4 * j + q // 2 + 2 * (q % 2)
+            w0 = off + q * nb + mi * P
+            for tq in range(4):
+                nc.tensor.matmul_mx(
+                    out=acc[(b0 // P + mi, n)][:, tq * P : (tq + 1) * P],
+                    lhsT=bcodes[:, w0 : w0 + P].bitcast(FP8X4),
+                    lhsT_scale=bscales[:, w0 : w0 + P],
+                    rhs=wcodes[:, 4 * n + tq, c, :].bitcast(FP8X4),
+                    rhs_scale=wplanes[4 * tq : P, n, c, :],
+                    start=(j == 0 and q == 0 and tq == 0),
+                    stop=(j == 3 and q == 3 and tq == 3),
+                )
 
-        done_units = 0
-        done_b = 0
-        for ci in range(n_chunks):
-            done_b += chunks[ci][3]
-            upto = min(64, int(64 * done_b / (W_DONE_AT * 16 * 256) + 0.999))
-            for q in range(done_units, upto):
-                w_unit(q)
-            before = done_units
-            done_units = upto
-            if chunks[ci][2] == 0:
-                state["sg"] = signs(chunks[ci][0], chunks[ci][1])
-            bases_chunk(ci, state["sg"])
+        def mx(count):
             for n in range(2):
-                need = 32 * (n + 1)
-                if done_units >= need:
-                    if before < need:
-                        for m in range(4):
-                            acc[(m, n)] = (accp if n == 0 else psum).tile(
-                                [P, 512], F32, tag=("acc%d" % m if n == 0 else "bank"), name="acc%d%d" % (m, n)
-                            )
-                        for cj in range(ci):
-                            mx(cj, n)
-                    mx(ci, n)
+                if not opened[n]:
+                    continue
+                while count and groups[n]:
+                    mx_group(n, *groups[n].pop(0))
+                    count -= 1
 
-        for m in range(4):
+        def mx_open(n):
+            for m in range(4):
+                acc[(m, n)] = (accp if n == 0 else psum).tile(
+                    [P, 512], F32, tag=("acc%d" % m if n == 0 else "bank"), name="acc%d%d" % (m, n)
+                )
+            opened[n] = True
+
+        w_at = {"t": 0, "g": 0, "q": 0}
+
+        def slot():
+            if w_at["q"] == 64:
+                mx(MX_LATE)
+                return
+            if w_at["t"] < 64:
+                w_transpose(w_at["t"])
+                w_at["t"] += 1
+            if w_at["g"] < 64 and (w_at["t"] == 64 or w_at["t"] - w_at["g"] > AHEAD_T):
+                w_gather(w_at["g"])
+                w_at["g"] += 1
+            if w_at["g"] == 64 or w_at["g"] - w_at["q"] > AHEAD_G:
+                w_quantise(w_at["q"])
+                w_at["q"] += 1
+                if w_at["q"] == 33:
+                    mx_open(0)
+                if w_at["q"] == 64:
+                    mx_open(1)
+            mx(MX_SLOT)
+
+        def store(m, n, on_act):
+            ost = state["ost"][:, m, n * 512 : (n + 1) * 512]
+            if on_act:
+                nc.scalar.copy(out=ost, in_=acc[(m, n)][:])
+            else:
+                nc.vector.tensor_copy(out=ost, in_=acc[(m, n)][:])
+            nc.sync.dma_start(out=out[m * P : (m + 1) * P, n * 512 : (n + 1) * 512], in_=ost)
+
+        with tc.manual_schedule(engines={mybir.EngineType.PE, mybir.EngineType.Activation, mybir.EngineType.DVE}):
+            sg, steps = signs(0)
+            for step in steps:
+                step()
+            for step in distances(0):
+                step()
+            fresh = []
+            for ci in range(n_chunks):
+                j, b0, nb, off = chunks[ci]
+                per_step = SLOTS * nb / 256 / 9.0
+
+                def slots():
+                    state["due"] = state.get("due", 0.0) + per_step
+                    while state["due"] >= 1.0:
+                        state["due"] -= 1.0
+                        slot()
+
+                ahead = distances(ci + 1) if ci + 1 < n_chunks else [lambda: None] * 7
+                next_sg, more = sg, [lambda: None] * 6
+                if ci + 1 < n_chunks and chunks[ci + 1][0] != j:
+                    next_sg, more = signs(j + 1)
+                inner_cubic, inner, outer, join, clamp, sign, split, quantise = values(ci, sg)
+                inner_cubic()
+                slots()
+                ahead[0]()
+                outer(0)
+                inner()
+                slots()
+                outer(1)
+                more[0]()
+                ahead[1]()
+                slots()
+                join(0)
+                more[1]()
+                ahead[2]()
+                slots()
+                join(1)
+                for n in range(2):
+                    groups[n].extend(fresh)
+                fresh = []
+                slots()
+                clamp()
+                more[2]()
+                ahead[3]()
+                slots()
+                sign()
+                more[3]()
+                ahead[4]()
+                slots()
+                split(0)
+                ahead[5]()
+                split(1)
+                more[4]()
+                slots()
+                quantise(0)
+                ahead[6]()
+                quantise(1)
+                more[5]()
+                slots()
+                fresh = [(ci, q, mi) for q in range(4) for mi in range(nb // P)]
+                sg = next_sg
+                if ci == n_chunks - 2:
+                    mx(1000)
+                    state["ost"] = raw.tile([P, 4, 1024], F32, tag="raw", name="ost")
+                    for m in range(2):
+                        for n in range(2):
+                            store(m, n, True)
             for n in range(2):
-                ost = ostp.tile([P, 512], F32)
-                if m < 3 or n == 0:
-                    nc.scalar.copy(out=ost[:], in_=acc[(m, n)][:])
-                else:
-                    nc.vector.tensor_copy(out=ost[:], in_=acc[(m, n)][:])
-                nc.sync.dma_start(out=out[m * P : (m + 1) * P, n * 512 : (n + 1) * 512], in_=ost[:])
+                groups[n].extend(fresh)
+            mx(1000)
+            for m in range(2, 4):
+                for n in range(2):
+                    store(m, n, n == 0)

@@ -20,8 +20,9 @@ FLOPS = 2 * B * K * OUT
 SLOTS = 12
 AHEAD_T = 3
 AHEAD_G = 2
-MX_SLOT = 2
-MX_LATE = 8
+MX_SLOT = 5
+RUN = 2
+MX_LATE = 32
 R6 = 6.0 ** -0.5
 
 
@@ -218,31 +219,32 @@ def tile_kanlinearnores_v2_kernel(tc, x, spline_weight, out):
 
             return inner_cubic, inner, outer, join, clamp, sign, split, quantise
 
-        acc = {}
-        groups = {0: [], 1: []}
+        acc, left = {}, {}
+        ready = {0: [], 1: []}
+        made = []
         opened = {0: False, 1: False}
 
-        def mx_group(n, ci, q, mi):
+        def mx_pass(t, ci, q, mi):
             j, b0, nb, off = chunks[ci]
+            n, tq = divmod(t, 4)
+            m = b0 // P + mi
             c = 4 * j + q // 2 + 2 * (q % 2)
             w0 = off + q * nb + mi * P
-            for tq in range(4):
-                nc.tensor.matmul_mx(
-                    out=acc[(b0 // P + mi, n)][:, tq * P : (tq + 1) * P],
-                    lhsT=bcodes[:, w0 : w0 + P].bitcast(FP8X4),
-                    lhsT_scale=bscales[:, w0 : w0 + P],
-                    rhs=wcodes[:, 4 * n + tq, c, :].bitcast(FP8X4),
-                    rhs_scale=wplanes[4 * tq : P, n, c, :],
-                    start=(j == 0 and q == 0 and tq == 0),
-                    stop=(j == 3 and q == 3 and tq == 3),
-                )
+            nc.tensor.matmul_mx(
+                out=acc[(m, n)][:, tq * P : (tq + 1) * P],
+                lhsT=bcodes[:, w0 : w0 + P].bitcast(FP8X4),
+                lhsT_scale=bscales[:, w0 : w0 + P],
+                rhs=wcodes[:, t, c, :].bitcast(FP8X4),
+                rhs_scale=wplanes[4 * tq : P, n, c, :],
+                start=left[(m, n)] == 64,
+                stop=left[(m, n)] == 1,
+            )
+            left[(m, n)] -= 1
 
         def mx(count):
             for n in range(2):
-                if not opened[n]:
-                    continue
-                while count and groups[n]:
-                    mx_group(n, *groups[n].pop(0))
+                while opened[n] and count > 0 and ready[n]:
+                    mx_pass(*ready[n].pop(0))
                     count -= 1
 
         def mx_open(n):
@@ -250,28 +252,56 @@ def tile_kanlinearnores_v2_kernel(tc, x, spline_weight, out):
                 acc[(m, n)] = (accp if n == 0 else psum).tile(
                     [P, 512], F32, tag=("acc%d" % m if n == 0 else "bank"), name="acc%d%d" % (m, n)
                 )
+                left[(m, n)] = 64
             opened[n] = True
 
-        w_at = {"t": 0, "g": 0, "q": 0}
+        def made_unit(q):
+            t, k = divmod(q, 8)
+            made.append(q)
+            for ci in state["chunks_made"]:
+                if chunks[ci][0] == k // 2:
+                    add(t, k, ci)
+
+        def add(t, k, ci):
+            for rp in range(2):
+                for mi in range(chunks[ci][2] // P):
+                    ready[t // 4].append((t, ci, 2 * rp + k % 2, mi))
+
+        def made_chunk(ci):
+            state["chunks_made"].append(ci)
+            for q in made:
+                t, k = divmod(q, 8)
+                if chunks[ci][0] == k // 2:
+                    add(t, k, ci)
+
+        w_at = {"t": 0, "g": 0, "q": 0, "slot": 0}
+        state["chunks_made"] = []
 
         def slot():
             if w_at["q"] == 64:
                 mx(MX_LATE)
                 return
-            if w_at["t"] < 64:
-                w_transpose(w_at["t"])
-                w_at["t"] += 1
-            if w_at["g"] < 64 and (w_at["t"] == 64 or w_at["t"] - w_at["g"] > AHEAD_T):
+            w_at["slot"] += 1
+            turn = w_at["slot"] % RUN == 0
+            if turn or w_at["t"] < AHEAD_T:
+                for i in range(RUN):
+                    if w_at["t"] < 64 and w_at["t"] - w_at["g"] < 4:
+                        w_transpose(w_at["t"])
+                        w_at["t"] += 1
+            if w_at["g"] < 64 and (w_at["t"] == 64 or w_at["t"] - w_at["g"] >= AHEAD_T):
                 w_gather(w_at["g"])
                 w_at["g"] += 1
             if w_at["g"] == 64 or w_at["g"] - w_at["q"] > AHEAD_G:
                 w_quantise(w_at["q"])
                 w_at["q"] += 1
-                if w_at["q"] == 33:
-                    mx_open(0)
+                if w_at["q"] > 2:
+                    made_unit(w_at["q"] - 3)
                 if w_at["q"] == 64:
+                    made_unit(62)
+                    made_unit(63)
                     mx_open(1)
-            mx(MX_SLOT)
+            if turn:
+                mx(MX_SLOT * RUN)
 
         def store(m, n, on_act):
             ost = state["ost"][:, m, n * 512 : (n + 1) * 512]
@@ -283,11 +313,11 @@ def tile_kanlinearnores_v2_kernel(tc, x, spline_weight, out):
 
         with tc.manual_schedule(engines={mybir.EngineType.PE, mybir.EngineType.Activation, mybir.EngineType.DVE}):
             sg, steps = signs(0)
+            mx_open(0)
             for step in steps:
                 step()
             for step in distances(0):
                 step()
-            fresh = []
             for ci in range(n_chunks):
                 j, b0, nb, off = chunks[ci]
                 per_step = SLOTS * nb / 256 / 9.0
@@ -318,9 +348,8 @@ def tile_kanlinearnores_v2_kernel(tc, x, spline_weight, out):
                 ahead[2]()
                 slots()
                 join(1)
-                for n in range(2):
-                    groups[n].extend(fresh)
-                fresh = []
+                if 0 < ci < n_chunks - 1:
+                    made_chunk(ci - 1)
                 slots()
                 clamp()
                 more[2]()
@@ -340,16 +369,15 @@ def tile_kanlinearnores_v2_kernel(tc, x, spline_weight, out):
                 quantise(1)
                 more[5]()
                 slots()
-                fresh = [(ci, q, mi) for q in range(4) for mi in range(nb // P)]
                 sg = next_sg
                 if ci == n_chunks - 2:
+                    made_chunk(ci)
                     mx(1000)
                     state["ost"] = raw.tile([P, 4, 1024], F32, tag="raw", name="ost")
                     for m in range(2):
                         for n in range(2):
                             store(m, n, True)
-            for n in range(2):
-                groups[n].extend(fresh)
+            made_chunk(n_chunks - 1)
             mx(1000)
             for m in range(2, 4):
                 for n in range(2):

@@ -17,11 +17,11 @@ K = IN * NB
 PASSES = K // 512
 FLOPS = 2 * B * K * OUT
 
-SLOTS = 12
+SLOTS = 11
+KAPPA = (1, 3, 5)
 AHEAD_T = 3
-AHEAD_G = 2
+AHEAD_G = 3
 MX_SLOT = 5
-RUN = 2
 MX_LATE = 32
 R6 = 6.0 ** -0.5
 
@@ -32,17 +32,18 @@ def tile_kanlinearnores_v2_kernel(tc, x, spline_weight, out):
     with ExitStack() as ctx:
         keep = ctx.enter_context(tc.tile_pool(name="keep", bufs=1))
         raw = ctx.enter_context(tc.tile_pool(name="raw", bufs=2))
-        wgp = ctx.enter_context(tc.tile_pool(name="wgp", bufs=4))
+        wgp = ctx.enter_context(tc.tile_pool(name="wgp", bufs=3))
         tmp = ctx.enter_context(tc.tile_pool(name="tmp", bufs=2))
+        tm1 = ctx.enter_context(tc.tile_pool(name="tm1", bufs=1))
         sgp = ctx.enter_context(tc.tile_pool(name="sgp", bufs=1))
         utp = ctx.enter_context(tc.tile_pool(name="utp", bufs=1))
+        ostp = ctx.enter_context(tc.tile_pool(name="ostp", bufs=4))
         sg2 = ctx.enter_context(tc.tile_pool(name="sg2", bufs=2))
-        psum = ctx.enter_context(tc.psum_pool(name="psum", bufs=4))
-        accp = ctx.enter_context(tc.psum_pool(name="accp", bufs=1))
+        psum = ctx.enter_context(tc.psum_pool(name="psum", bufs=1))
 
         ident = keep.tile([P, P], F32)
         wcodes = keep.tile([P, 8, PASSES, P], U32, align_bytes=64)
-        wplanes = keep.tile([P, 2, PASSES, P], U8, align_bytes=64)
+        wplanes = keep.tile([P, 4, PASSES, P], U8, align_bytes=64)
         bcodes = keep.tile([P, PASSES * B], U32, align_bytes=64)
         bscales = keep.tile([P, PASSES * B], U8, align_bytes=64)
         xt = keep.tile([P, 4 * B * 2], BF16, align_bytes=64)
@@ -55,17 +56,20 @@ def tile_kanlinearnores_v2_kernel(tc, x, spline_weight, out):
         xwords = xr[:, 0 : 4 * IN].bitcast(F32).rearrange("p (t q s) -> p t q s", t=4, s=4)
         xt_words = xt[:].bitcast(F32)
         xt_jb = xt_words.rearrange("p (j b) -> p j b", j=4)
-        xbanks = [[psum.tile([P, 512], F32, tag="bank", name="xbank%d%d" % (jh, bh)) for bh in range(2)] for jh in range(2)]
+        xbanks = [
+            [psum.tile([P, 512], F32, tag="bank%d" % (4 + 2 * jh + bh), name="xbank%d%d" % (jh, bh)) for bh in range(2)]
+            for jh in range(2)
+        ]
         for bt in range(4):
             for j in range(4):
                 col = (j % 2) * 256 + (bt % 2) * P
                 nc.tensor.transpose(
                     out=xbanks[j // 2][bt // 2][:, col : col + P], in_=xwords[:, bt, :, j], identity=ident[:]
                 )
-        for bh in range(2):
+        def x_copy(b0, b1):
             for jh in range(2):
-                dst = xt_jb[:, 2 * jh : 2 * jh + 2, bh * 256 : (bh + 1) * 256]
-                src = xbanks[jh][bh][:].rearrange("p (j b) -> p j b", j=2)
+                dst = xt_jb[:, 2 * jh : 2 * jh + 2, b0:b1]
+                src = xbanks[jh][b0 // 256][:].rearrange("p (j b) -> p j b", j=2)[:, :, b0 % 256 : b0 % 256 + b1 - b0]
                 if jh == 0:
                     nc.scalar.copy(out=dst, in_=src)
                 else:
@@ -74,14 +78,20 @@ def tile_kanlinearnores_v2_kernel(tc, x, spline_weight, out):
         state = {}
         banks, gathers = {}, {}
 
+        def w_load(t):
+            wr = raw.tile([P, K], BF16, tag="raw")
+            nc.sync.dma_start(out=wr[:], in_=w2d[t * P : (t + 1) * P, :])
+            state["next"] = wr[:].bitcast(F32).rearrange("p (q s) -> p q s", s=32)
+
         def w_transpose(q):
             t, k = divmod(q, 8)
             if k == 0:
-                wr = raw.tile([P, K], BF16, tag="raw")
-                nc.sync.dma_start(out=wr[:], in_=w2d[t * P : (t + 1) * P, :])
-                state["words"] = wr[:].bitcast(F32).rearrange("p (q s) -> p q s", s=32)
+                state["words"] = state["next"]
+                if t < 7:
+                    w_load(t + 1)
             words = state["words"]
-            bank = psum.tile([P, 512], F32, tag="bank")
+            free = 8 - w_at["first"]
+            bank = psum.tile([P, 512], F32, tag="bank%d" % (w_at["first"] + q % free), name="wbank%d" % q)
             for cc in range(2):
                 c = 2 * k + cc
                 for u in range(2):
@@ -95,36 +105,41 @@ def tile_kanlinearnores_v2_kernel(tc, x, spline_weight, out):
 
         def w_gather(q):
             bank = banks.pop(q)
-            wg = wgp.tile([P, 1024], BF16, align_bytes=64)
+            if q % 2 == 0:
+                gathers[q // 2] = wgp.tile([P, 2048], BF16, align_bytes=64, name="wg")
+            wg = gathers[q // 2][:, q % 2 * 1024 : (q % 2 + 1) * 1024]
             nc.scalar.copy(
-                out=wg[:].bitcast(F32).rearrange("p (c o u) -> p c o u", c=2, u=2),
+                out=wg.bitcast(F32).rearrange("p (c o u) -> p c o u", c=2, u=2),
                 in_=bank[:].rearrange("p (c u o) -> p c o u", c=2, u=2),
             )
-            gathers[q] = wg
 
         def w_quantise(q):
-            t, k = divmod(q, 8)
+            t, k = divmod(q, 4)
             wg = gathers.pop(q)
             nc.vector.quantize_mx(
-                out=wcodes[:, t, 2 * k : 2 * k + 2, :].rearrange("p c o -> p (c o)").bitcast(FP8X4),
-                scales=wplanes[4 * (t % 4) : P, t // 4, 2 * k : 2 * k + 2, :].rearrange("p c o -> p (c o)"),
+                out=wcodes[:, t, 4 * k : 4 * k + 4, :].rearrange("p c o -> p (c o)").bitcast(FP8X4),
+                scales=wplanes[4 * (t % 2) : P, t // 2, 4 * k : 4 * k + 4, :].rearrange("p c o -> p (c o)"),
                 in_=wg[:],
             )
 
         chunks = []
-        for j in range(4):
-            sizes = {0: (128, 128, 256), 3: (256, 128, 128)}.get(j, (256, 256))
-            b0 = 0
-            for nb in sizes:
-                chunks.append((j, b0, nb, 4 * (j * B + b0)))
-                b0 += nb
+        for half in range(2):
+            for j in range(4):
+                sizes = (128, 128) if (half, j) in ((0, 0), (1, 3)) else (256,)
+                b0 = 256 * half
+                for nb in sizes:
+                    chunks.append((j, b0, nb, 4 * (j * B + b0)))
+                    b0 += nb
         n_chunks = len(chunks)
 
-        def signs(j):
-            xs = xt[:, j * 1024 : (j + 1) * 1024]
-            yt = sgp.tile([P, 1024, 2], BF16, tag="yt")
-            sgt = sg2.tile([P, 2, 2048], BF16, tag="sgt")
-            y = yt[:].rearrange("p n e -> p (n e)")
+        def signs(ci):
+            j, b0, nb, off = chunks[ci]
+            n = 2 * nb
+            xs = xt[:, j * 1024 + 2 * b0 : j * 1024 + 2 * b0 + n]
+            ytt = sgp.tile([P, 512, 2], BF16, tag="yt")
+            sgtt = sg2.tile([P, 2, 1024], BF16, tag="sgt")
+            yt, sgt = ytt[:, 0:n, :], sgtt[:, :, 0 : 2 * n]
+            y = yt.rearrange("p n e -> p (n e)")
             return sgt, [
                 lambda: nc.vector.tensor_copy(out=yt[:, :, 0], in_=xs),
                 lambda: nc.vector.tensor_scalar_add(out=yt[:, :, 1], in0=xs, scalar1=-0.4),
@@ -132,10 +147,10 @@ def tile_kanlinearnores_v2_kernel(tc, x, spline_weight, out):
                     out=sgt[:, 0, :], in0=y, scalar1=-0.6, scalar2=0.5, op0=ALU.is_ge, op1=ALU.subtract
                 ),
                 lambda: nc.vector.tensor_scalar(
-                    out=sgt[:, 1, :], in0=y, scalar1=0.2, scalar2=1.0, op0=ALU.is_ge, op1=ALU.mult
+                    out=sgt[:, 1, :], in0=y, scalar1=0.2, scalar2=-1.0 if ci in KAPPA else 1.0, op0=ALU.is_ge, op1=ALU.mult
                 ),
                 lambda: nc.vector.tensor_scalar(
-                    out=y, in0=y, scalar1=-1.402, scalar2=-0.5, op0=ALU.is_ge, op1=ALU.mult
+                    out=y, in0=y, scalar1=-1.402, scalar2=0.5 if ci in KAPPA else -0.5, op0=ALU.is_ge, op1=ALU.mult
                 ),
                 lambda: nc.vector.tensor_tensor(out=sgt[:, 1, :], in0=sgt[:, 1, :], in1=y, op=ALU.add),
             ]
@@ -146,10 +161,10 @@ def tile_kanlinearnores_v2_kernel(tc, x, spline_weight, out):
             xs = xt[:, j * 1024 + 2 * b0 : j * 1024 + 2 * b0 + n]
             td = tmp.tile([P, 2, 512], F32, tag="td")
             td2 = tmp.tile([P, 2, 512], F32, tag="td2")
-            ta = tmp.tile([P, 2, 512], F32, tag="ta")
-            tb = tmp.tile([P, 2, 512], F32, tag="tb")
-            th = tmp.tile([P, 2, 512], F32, tag="th")
-            tw = tmp.tile([P, 2, 512], F32, tag="tw")
+            ta = tm1.tile([P, 2, 512], F32, tag="ta")
+            tb = tm1.tile([P, 2, 512], F32, tag="tb")
+            th = tm1.tile([P, 2, 512], F32, tag="th")
+            tw = tm1.tile([P, 2, 512], F32, tag="tw")
             d0, d2, sa, sb, h, w2 = (t[:, :, 0:n] for t in (td, td2, ta, tb, th, tw))
             state[ci] = (d0, d2, sa, sb, h, w2)
 
@@ -157,6 +172,17 @@ def tile_kanlinearnores_v2_kernel(tc, x, spline_weight, out):
                 for e in range(2):
                     nc.scalar.activation(out=td[:, e, 0:n], in_=xs, func=ACT.Abs, bias=1.5 - e, scale=2.5)
 
+            if ci in KAPPA:
+                r23 = (2.0 / 3.0) ** 0.5
+                return [
+                    first,
+                    lambda: nc.scalar.activation(out=d0, in_=d0, func=ACT.Abs, bias=-2.0, scale=1.0),
+                    lambda: nc.scalar.activation(out=d2, in_=d0, func=ACT.Abs, bias=-2.0, scale=1.0),
+                    lambda: nc.scalar.activation(out=w2, in_=d2, func=ACT.Square, bias=-r23, scale=r23),
+                    lambda: nc.scalar.activation(out=sa, in_=d2, func=ACT.Square, scale=R6),
+                    lambda: nc.scalar.activation(out=sb, in_=d2, func=ACT.Square, bias=2.0 * R6, scale=-R6),
+                    lambda: None,
+                ]
             return [
                 first,
                 lambda: nc.scalar.activation(out=d0, in_=d0, func=ACT.Abs, bias=-2.0, scale=1.0),
@@ -171,18 +197,24 @@ def tile_kanlinearnores_v2_kernel(tc, x, spline_weight, out):
             j, b0, nb, off = chunks[ci]
             n = 2 * nb
             d0, d2, sa, sb, h, w2 = state.pop(ci)
-            ngt = sgp.tile([P, 1024], BF16, tag="ng")
+            ngt = sgp.tile([P, 1, 1024], BF16, tag="ng")
             ut = utp.tile([P, 2, 1024], BF16, tag="ut")
             ob = sgp.tile([P, 4096], BF16, tag="ob", align_bytes=64)
-            ng = ngt[:, 0 : 2 * n]
+            ng = ngt[:, 0, 0 : 2 * n]
+            kap = ci in KAPPA
             u = [ut[:, r, 0 : 2 * n] for r in range(2)]
             both = ut[:, :, 0 : 2 * n]
             humps = ob[:, 0 : 8 * n].rearrange("p (r h n) -> p r h n", r=2, h=2)
 
             def inner_cubic():
+                if kap:
+                    nc.vector.scalar_tensor_tensor(out=w2, in0=d2, scalar=1.0, in1=w2, op0=ALU.subtract, op1=ALU.mult)
+                    return
                 nc.vector.scalar_tensor_tensor(out=w2, in0=h, scalar=1.0, in1=w2, op0=ALU.add, op1=ALU.mult)
 
             def inner():
+                if kap:
+                    return
                 nc.scalar.activation(
                     out=ng.rearrange("p (n e) -> p n e", e=2), in_=w2.rearrange("p e n -> p n e"),
                     func=ACT.Identity, bias=-2.0 / 3.0, scale=0.5,
@@ -190,19 +222,35 @@ def tile_kanlinearnores_v2_kernel(tc, x, spline_weight, out):
 
             def outer(r):
                 dist, sq = ((d0, sa), (d2, sb))[r]
+                if kap:
+                    nc.vector.scalar_tensor_tensor(out=sq, in0=dist, scalar=2.0, in1=sq, op0=ALU.subtract, op1=ALU.mult)
+                    return
                 nc.vector.scalar_tensor_tensor(
                     out=u[r].rearrange("p (n e) -> p n e", e=2), in0=dist.rearrange("p e n -> p n e"), scalar=2.0,
                     in1=sq.rearrange("p e n -> p n e"), op0=ALU.subtract, op1=ALU.mult,
                 )
 
             def join(r):
-                nc.vector.tensor_tensor(out=u[r], in0=u[r], in1=ng, op=ALU.max)
+                if kap:
+                    nc.vector.scalar_tensor_tensor(
+                        out=u[r].rearrange("p (n e) -> p n e", e=2), in0=w2.rearrange("p e n -> p n e"), scalar=0.0,
+                        in1=(sa, sb)[r].rearrange("p e n -> p n e"),
+                        op0=(ALU.max, ALU.min)[r], op1=(ALU.add, ALU.subtract)[r],
+                    )
+                elif r == 1:
+                    nc.vector.tensor_tensor(
+                        out=both, in0=both, in1=ngt[:, :, 0 : 2 * n].to_broadcast([P, 2, 2 * n]), op=ALU.max
+                    )
 
             def clamp():
+                if kap:
+                    nc.vector.tensor_scalar_min(out=u[0], in0=u[0], scalar1=0.0)
+                    nc.vector.tensor_scalar_max(out=u[1], in0=u[1], scalar1=0.0)
+                    return
                 nc.vector.tensor_scalar_min(out=both, in0=both, scalar1=0.0)
 
             def sign():
-                nc.vector.tensor_tensor(out=both, in0=both, in1=sgt[:, :, 4 * b0 : 4 * (b0 + nb)], op=ALU.mult)
+                nc.vector.tensor_tensor(out=both, in0=both, in1=sgt, op=ALU.mult)
 
             def split(hh):
                 nc.vector.tensor_scalar(
@@ -210,6 +258,14 @@ def tile_kanlinearnores_v2_kernel(tc, x, spline_weight, out):
                 )
 
             def quantise(r):
+                if nb == 256:
+                    if r == 1:
+                        nc.vector.quantize_mx(
+                            out=bcodes[:, off : off + 4 * nb].bitcast(FP8X4),
+                            scales=bscales[:, off : off + 4 * nb],
+                            in_=ob[:, 0 : 8 * n],
+                        )
+                    return
                 w0 = off + r * 2 * nb
                 nc.vector.quantize_mx(
                     out=bcodes[:, w0 : w0 + 2 * nb].bitcast(FP8X4),
@@ -220,9 +276,9 @@ def tile_kanlinearnores_v2_kernel(tc, x, spline_weight, out):
             return inner_cubic, inner, outer, join, clamp, sign, split, quantise
 
         acc, left = {}, {}
-        ready = {0: [], 1: []}
+        ready = {}
         made = []
-        opened = {0: False, 1: False}
+        state["chunks_made"] = []
 
         def mx_pass(t, ci, q, mi):
             j, b0, nb, off = chunks[ci]
@@ -235,89 +291,95 @@ def tile_kanlinearnores_v2_kernel(tc, x, spline_weight, out):
                 lhsT=bcodes[:, w0 : w0 + P].bitcast(FP8X4),
                 lhsT_scale=bscales[:, w0 : w0 + P],
                 rhs=wcodes[:, t, c, :].bitcast(FP8X4),
-                rhs_scale=wplanes[4 * tq : P, n, c, :],
+                rhs_scale=wplanes[4 * (t % 2) : P, t // 2, c, :],
                 start=left[(m, n)] == 64,
                 stop=left[(m, n)] == 1,
             )
             left[(m, n)] -= 1
 
         def mx(count):
-            for n in range(2):
-                while opened[n] and count > 0 and ready[n]:
-                    mx_pass(*ready[n].pop(0))
+            for key in sorted(ready):
+                while key in acc and count > 0 and ready[key]:
+                    mx_pass(*ready[key].pop(0))
                     count -= 1
 
-        def mx_open(n):
-            for m in range(4):
-                acc[(m, n)] = (accp if n == 0 else psum).tile(
-                    [P, 512], F32, tag=("acc%d" % m if n == 0 else "bank"), name="acc%d%d" % (m, n)
-                )
+        def mx_open(half, n):
+            for m in range(2 * half, 2 * half + 2):
+                acc[(m, n)] = psum.tile([P, 512], F32, tag="bank%d" % (4 * half + 2 * n + m % 2), name="acc%d%d" % (m, n))
                 left[(m, n)] = 64
-            opened[n] = True
+                ready.setdefault((m, n), [])
 
         def made_unit(q):
-            t, k = divmod(q, 8)
             made.append(q)
             for ci in state["chunks_made"]:
-                if chunks[ci][0] == k // 2:
-                    add(t, k, ci)
+                add(q, ci)
 
-        def add(t, k, ci):
-            for rp in range(2):
+        def add(q, ci, rs=(0, 1, 2, 3)):
+            t, j = divmod(q, 4)
+            if chunks[ci][0] == j:
                 for mi in range(chunks[ci][2] // P):
-                    ready[t // 4].append((t, ci, 2 * rp + k % 2, mi))
+                    todo = ready.setdefault((chunks[ci][1] // P + mi, t // 4), [])
+                    todo.extend((t, ci, r, mi) for r in rs)
 
         def made_chunk(ci):
             state["chunks_made"].append(ci)
-            for q in made:
-                t, k = divmod(q, 8)
-                if chunks[ci][0] == k // 2:
-                    add(t, k, ci)
+            for rs in ((0, 1), (2, 3)):
+                for q in made:
+                    add(q, ci, rs)
 
-        w_at = {"t": 0, "g": 0, "q": 0, "slot": 0}
-        state["chunks_made"] = []
+        w_at = {"t": 0, "g": 0, "q": 0, "first": 4}
 
         def slot():
-            if w_at["q"] == 64:
+            if w_at["q"] == 32:
                 mx(MX_LATE)
                 return
-            w_at["slot"] += 1
-            turn = w_at["slot"] % RUN == 0
-            if turn or w_at["t"] < AHEAD_T:
-                for i in range(RUN):
-                    if w_at["t"] < 64 and w_at["t"] - w_at["g"] < 4:
-                        w_transpose(w_at["t"])
-                        w_at["t"] += 1
-            if w_at["g"] < 64 and (w_at["t"] == 64 or w_at["t"] - w_at["g"] >= AHEAD_T):
+            if w_at["t"] < 64 and w_at["t"] - w_at["g"] < 8 - w_at["first"]:
+                w_transpose(w_at["t"])
+                w_at["t"] += 1
+            if w_at["g"] < 64 and (w_at["t"] == 64 or w_at["t"] - w_at["g"] >= min(AHEAD_T, 8 - w_at["first"])):
                 w_gather(w_at["g"])
                 w_at["g"] += 1
-            if w_at["g"] == 64 or w_at["g"] - w_at["q"] > AHEAD_G:
+            if w_at["g"] == 64 or w_at["g"] - 2 * w_at["q"] > AHEAD_G:
                 w_quantise(w_at["q"])
                 w_at["q"] += 1
-                if w_at["q"] > 2:
-                    made_unit(w_at["q"] - 3)
-                if w_at["q"] == 64:
-                    made_unit(62)
-                    made_unit(63)
-                    mx_open(1)
-            if turn:
-                mx(MX_SLOT * RUN)
+                if w_at["q"] > 1:
+                    made_unit(w_at["q"] - 2)
+                if w_at["q"] == 32:
+                    made_unit(31)
+                    mx_open(1, 1)
+            mx(MX_SLOT)
 
         def store(m, n, on_act):
-            ost = state["ost"][:, m, n * 512 : (n + 1) * 512]
+            ostt = ostp.tile([P, 512], F32, name="ost")
+            ost = ostt[:]
             if on_act:
                 nc.scalar.copy(out=ost, in_=acc[(m, n)][:])
             else:
                 nc.vector.tensor_copy(out=ost, in_=acc[(m, n)][:])
             nc.sync.dma_start(out=out[m * P : (m + 1) * P, n * 512 : (n + 1) * 512], in_=ost)
 
+        def stores():
+            for m in range(4):
+                for n in range(2):
+                    if left.get((m, n)) == 0:
+                        left[(m, n)] = -1
+                        store(m, n, m < 3 or n == 0)
+
         with tc.manual_schedule(engines={mybir.EngineType.PE, mybir.EngineType.Activation, mybir.EngineType.DVE}):
+            w_load(0)
             sg, steps = signs(0)
-            mx_open(0)
+            mx_open(0, 0)
+            mx_open(0, 1)
+            x_copy(0, P)
+            first = distances(0)
+            for step in first[:2]:
+                step()
             for step in steps:
                 step()
-            for step in distances(0):
+            x_copy(P, 256)
+            for step in first[2:]:
                 step()
+            x_copy(256, B)
             for ci in range(n_chunks):
                 j, b0, nb, off = chunks[ci]
                 per_step = SLOTS * nb / 256 / 9.0
@@ -328,10 +390,10 @@ def tile_kanlinearnores_v2_kernel(tc, x, spline_weight, out):
                         state["due"] -= 1.0
                         slot()
 
-                ahead = distances(ci + 1) if ci + 1 < n_chunks else [lambda: None] * 7
-                next_sg, more = sg, [lambda: None] * 6
-                if ci + 1 < n_chunks and chunks[ci + 1][0] != j:
-                    next_sg, more = signs(j + 1)
+                ahead, next_sg, more = [lambda: None] * 7, sg, [lambda: None] * 6
+                if ci + 1 < n_chunks:
+                    ahead = distances(ci + 1)
+                    next_sg, more = signs(ci + 1)
                 inner_cubic, inner, outer, join, clamp, sign, split, quantise = values(ci, sg)
                 inner_cubic()
                 slots()
@@ -348,8 +410,14 @@ def tile_kanlinearnores_v2_kernel(tc, x, spline_weight, out):
                 ahead[2]()
                 slots()
                 join(1)
-                if 0 < ci < n_chunks - 1:
+                if ci > 0:
                     made_chunk(ci - 1)
+                    if chunks[ci - 1][1] == 256 and w_at["first"] == 4:
+                        w_at["first"] = 6
+                        state["open"] = w_at["t"]
+                if state.get("open") is not None and w_at["g"] >= state["open"]:
+                    state["open"] = None
+                    mx_open(1, 0)
                 slots()
                 clamp()
                 more[2]()
@@ -370,15 +438,9 @@ def tile_kanlinearnores_v2_kernel(tc, x, spline_weight, out):
                 more[5]()
                 slots()
                 sg = next_sg
-                if ci == n_chunks - 2:
-                    made_chunk(ci)
-                    mx(1000)
-                    state["ost"] = raw.tile([P, 4, 1024], F32, tag="raw", name="ost")
-                    for m in range(2):
-                        for n in range(2):
-                            store(m, n, True)
-            made_chunk(n_chunks - 1)
-            mx(1000)
-            for m in range(2, 4):
-                for n in range(2):
-                    store(m, n, n == 0)
+                stores()
+            for rs in ((0, 1), (2, 3)):
+                for q in made:
+                    add(q, n_chunks - 1, rs)
+                mx(1000)
+            stores()

@@ -17,12 +17,17 @@ K = IN * NB
 PASSES = K // 512
 FLOPS = 2 * B * K * OUT
 
-SLOTS = 11
-KAPPA = (1, 3, 5)
+SLOTS = 12
+FRONT = 4
+SLOTS_B = 10
+KAPPA = (0, 1, 2, 3)
 AHEAD_T = 3
 AHEAD_G = 3
-MX_SLOT = 5
-MX_LATE = 32
+MX_SLOT = 12
+RUN = 1
+MX_LATE = 64
+Y_ACT = (8, 9)
+S_ACT = ()
 R6 = 6.0 ** -0.5
 
 
@@ -141,8 +146,12 @@ def tile_kanlinearnores_v2_kernel(tc, x, spline_weight, out):
             yt, sgt = ytt[:, 0:n, :], sgtt[:, :, 0 : 2 * n]
             y = yt.rearrange("p n e -> p (n e)")
             return sgt, [
-                lambda: nc.vector.tensor_copy(out=yt[:, :, 0], in_=xs),
-                lambda: nc.vector.tensor_scalar_add(out=yt[:, :, 1], in0=xs, scalar1=-0.4),
+                lambda: nc.scalar.copy(out=yt[:, :, 0], in_=xs)
+                if ci in Y_ACT
+                else nc.vector.tensor_copy(out=yt[:, :, 0], in_=xs),
+                lambda: nc.scalar.activation(out=yt[:, :, 1], in_=xs, func=ACT.Identity, bias=-0.4)
+                if ci in Y_ACT
+                else nc.vector.tensor_scalar_add(out=yt[:, :, 1], in0=xs, scalar1=-0.4),
                 lambda: nc.vector.tensor_scalar(
                     out=sgt[:, 0, :], in0=y, scalar1=-0.6, scalar2=0.5, op0=ALU.is_ge, op1=ALU.subtract
                 ),
@@ -253,6 +262,9 @@ def tile_kanlinearnores_v2_kernel(tc, x, spline_weight, out):
                 nc.vector.tensor_tensor(out=both, in0=both, in1=sgt, op=ALU.mult)
 
             def split(hh):
+                if hh == 1 and ci in S_ACT:
+                    nc.scalar.activation(out=humps[:, :, hh, :], in_=both, func=ACT.Relu, scale=-2.0)
+                    return
                 nc.vector.tensor_scalar(
                     out=humps[:, :, hh, :], in0=both, scalar1=(2.0, -2.0)[hh], scalar2=0.0, op0=ALU.mult, op1=ALU.max
                 )
@@ -273,7 +285,27 @@ def tile_kanlinearnores_v2_kernel(tc, x, spline_weight, out):
                     in_=ob[:, r * 4 * n : (r + 1) * 4 * n],
                 )
 
-            return inner_cubic, inner, outer, join, clamp, sign, split, quantise
+            def finish():
+                if ci > 0:
+                    made_chunk(ci - 1)
+                for r in range(2):
+                    nc.vector.tensor_tensor(out=u[r], in0=u[r], in1=ng, op=ALU.max)
+                    mx(MX_LATE)
+                    nc.vector.tensor_scalar_min(out=u[r], in0=u[r], scalar1=0.0)
+                    nc.vector.tensor_tensor(out=u[r], in0=u[r], in1=sgt[:, r, :], op=ALU.mult)
+                    for hh in range(2):
+                        nc.vector.tensor_scalar(
+                            out=humps[:, r, hh, :], in0=u[r], scalar1=(2.0, -2.0)[hh], scalar2=0.0,
+                            op0=ALU.mult, op1=ALU.max,
+                        )
+                    quantise(r)
+                    stores()
+                    for q in made:
+                        add(q, ci, (2 * r, 2 * r + 1))
+                    mx(1000)
+                stores()
+
+            return inner_cubic, inner, outer, join, clamp, sign, split, quantise, finish
 
         acc, left = {}, {}
         ready = {}
@@ -305,7 +337,7 @@ def tile_kanlinearnores_v2_kernel(tc, x, spline_weight, out):
 
         def mx_open(half, n):
             for m in range(2 * half, 2 * half + 2):
-                acc[(m, n)] = psum.tile([P, 512], F32, tag="bank%d" % (4 * half + 2 * n + m % 2), name="acc%d%d" % (m, n))
+                acc[(m, n)] = psum.tile([P, 512], F32, tag="bank%d" % ((0, 2, 4, 0)[2 * half + n] + m % 2), name="acc%d%d" % (m, n))
                 left[(m, n)] = 64
                 ready.setdefault((m, n), [])
 
@@ -327,16 +359,20 @@ def tile_kanlinearnores_v2_kernel(tc, x, spline_weight, out):
                 for q in made:
                     add(q, ci, rs)
 
-        w_at = {"t": 0, "g": 0, "q": 0, "first": 4}
+        w_at = {"t": 0, "g": 0, "q": 0, "first": 4, "slot": 0}
 
         def slot():
             if w_at["q"] == 32:
                 mx(MX_LATE)
                 return
-            if w_at["t"] < 64 and w_at["t"] - w_at["g"] < 8 - w_at["first"]:
-                w_transpose(w_at["t"])
-                w_at["t"] += 1
-            if w_at["g"] < 64 and (w_at["t"] == 64 or w_at["t"] - w_at["g"] >= min(AHEAD_T, 8 - w_at["first"])):
+            w_at["slot"] += 1
+            turn = w_at["slot"] % RUN == 0
+            if turn or w_at["t"] < RUN:
+                for i in range(RUN):
+                    if w_at["t"] < 64 and w_at["t"] - w_at["g"] < 8 - w_at["first"]:
+                        w_transpose(w_at["t"])
+                        w_at["t"] += 1
+            if w_at["g"] < 64 and w_at["g"] < w_at["t"] and (w_at["t"] == 64 or w_at["t"] - w_at["g"] >= min(AHEAD_T, 8 - w_at["first"] - RUN + 1)):
                 w_gather(w_at["g"])
                 w_at["g"] += 1
             if w_at["g"] == 64 or w_at["g"] - 2 * w_at["q"] > AHEAD_G:
@@ -346,8 +382,8 @@ def tile_kanlinearnores_v2_kernel(tc, x, spline_weight, out):
                     made_unit(w_at["q"] - 2)
                 if w_at["q"] == 32:
                     made_unit(31)
-                    mx_open(1, 1)
-            mx(MX_SLOT)
+            if turn:
+                mx(MX_SLOT * RUN)
 
         def store(m, n, on_act):
             ostt = ostp.tile([P, 512], F32, name="ost")
@@ -364,6 +400,8 @@ def tile_kanlinearnores_v2_kernel(tc, x, spline_weight, out):
                     if left.get((m, n)) == 0:
                         left[(m, n)] = -1
                         store(m, n, m < 3 or n == 0)
+            if left[(0, 0)] == left[(1, 0)] == -1 and (2, 1) not in acc:
+                mx_open(1, 1)
 
         with tc.manual_schedule(engines={mybir.EngineType.PE, mybir.EngineType.Activation, mybir.EngineType.DVE}):
             w_load(0)
@@ -380,9 +418,10 @@ def tile_kanlinearnores_v2_kernel(tc, x, spline_weight, out):
             for step in first[2:]:
                 step()
             x_copy(256, B)
+            late = None
             for ci in range(n_chunks):
                 j, b0, nb, off = chunks[ci]
-                per_step = SLOTS * nb / 256 / 9.0
+                per_step = (SLOTS if ci < FRONT else SLOTS_B) * nb / 256 / 9.0
 
                 def slots():
                     state["due"] = state.get("due", 0.0) + per_step
@@ -394,17 +433,24 @@ def tile_kanlinearnores_v2_kernel(tc, x, spline_weight, out):
                 if ci + 1 < n_chunks:
                     ahead = distances(ci + 1)
                     next_sg, more = signs(ci + 1)
-                inner_cubic, inner, outer, join, clamp, sign, split, quantise = values(ci, sg)
+                inner_cubic, inner, outer, join, clamp, sign, split, quantise, finish = values(ci, sg)
                 inner_cubic()
                 slots()
                 ahead[0]()
                 outer(0)
+                if late is not None:
+                    late(0)
+                    late(1)
+                    late = None
                 inner()
                 slots()
                 outer(1)
                 more[0]()
                 ahead[1]()
                 slots()
+                if ci == n_chunks - 1:
+                    finish()
+                    break
                 join(0)
                 more[1]()
                 ahead[2]()
@@ -429,18 +475,19 @@ def tile_kanlinearnores_v2_kernel(tc, x, spline_weight, out):
                 slots()
                 split(0)
                 ahead[5]()
-                split(1)
+                if ci not in S_ACT:
+                    split(1)
                 more[4]()
                 slots()
-                quantise(0)
+                if ci not in S_ACT:
+                    quantise(0)
                 ahead[6]()
-                quantise(1)
+                if ci in S_ACT:
+                    split(1)
+                    late = quantise
+                else:
+                    quantise(1)
                 more[5]()
                 slots()
                 sg = next_sg
                 stores()
-            for rs in ((0, 1), (2, 3)):
-                for q in made:
-                    add(q, n_chunks - 1, rs)
-                mx(1000)
-            stores()

@@ -27,7 +27,6 @@ MX_SLOT = 12
 RUN = 1
 MX_LATE = 64
 Y_ACT = (8, 9)
-S_ACT = ()
 R6 = 6.0 ** -0.5
 
 
@@ -212,7 +211,6 @@ def tile_kanlinearnores_v2_kernel(tc, x, spline_weight, out):
             ng = ngt[:, 0, 0 : 2 * n]
             kap = ci in KAPPA
             u = [ut[:, r, 0 : 2 * n] for r in range(2)]
-            both = ut[:, :, 0 : 2 * n]
             humps = ob[:, 0 : 8 * n].rearrange("p (r h n) -> p r h n", r=2, h=2)
 
             def inner_cubic():
@@ -246,38 +244,25 @@ def tile_kanlinearnores_v2_kernel(tc, x, spline_weight, out):
                         in1=(sa, sb)[r].rearrange("p e n -> p n e"),
                         op0=(ALU.max, ALU.min)[r], op1=(ALU.add, ALU.subtract)[r],
                     )
-                elif r == 1:
-                    nc.vector.tensor_tensor(
-                        out=both, in0=both, in1=ngt[:, :, 0 : 2 * n].to_broadcast([P, 2, 2 * n]), op=ALU.max
+                else:
+                    nc.vector.tensor_tensor(out=u[r], in0=u[r], in1=ng, op=ALU.max)
+
+            def clamp(r):
+                if kap and r == 1:
+                    nc.vector.tensor_scalar_max(out=u[1], in0=u[1], scalar1=0.0)
+                else:
+                    nc.vector.tensor_scalar_min(out=u[r], in0=u[r], scalar1=0.0)
+
+            def sign(r):
+                nc.vector.tensor_tensor(out=u[r], in0=u[r], in1=sgt[:, r, :], op=ALU.mult)
+
+            def split(r):
+                for hh in range(2):
+                    nc.vector.tensor_scalar(
+                        out=humps[:, r, hh, :], in0=u[r], scalar1=(2.0, -2.0)[hh], scalar2=0.0, op0=ALU.mult, op1=ALU.max
                     )
 
-            def clamp():
-                if kap:
-                    nc.vector.tensor_scalar_min(out=u[0], in0=u[0], scalar1=0.0)
-                    nc.vector.tensor_scalar_max(out=u[1], in0=u[1], scalar1=0.0)
-                    return
-                nc.vector.tensor_scalar_min(out=both, in0=both, scalar1=0.0)
-
-            def sign():
-                nc.vector.tensor_tensor(out=both, in0=both, in1=sgt, op=ALU.mult)
-
-            def split(hh):
-                if hh == 1 and ci in S_ACT:
-                    nc.scalar.activation(out=humps[:, :, hh, :], in_=both, func=ACT.Relu, scale=-2.0)
-                    return
-                nc.vector.tensor_scalar(
-                    out=humps[:, :, hh, :], in0=both, scalar1=(2.0, -2.0)[hh], scalar2=0.0, op0=ALU.mult, op1=ALU.max
-                )
-
             def quantise(r):
-                if nb == 256:
-                    if r == 1:
-                        nc.vector.quantize_mx(
-                            out=bcodes[:, off : off + 4 * nb].bitcast(FP8X4),
-                            scales=bscales[:, off : off + 4 * nb],
-                            in_=ob[:, 0 : 8 * n],
-                        )
-                    return
                 w0 = off + r * 2 * nb
                 nc.vector.quantize_mx(
                     out=bcodes[:, w0 : w0 + 2 * nb].bitcast(FP8X4),
@@ -291,13 +276,9 @@ def tile_kanlinearnores_v2_kernel(tc, x, spline_weight, out):
                 for r in range(2):
                     nc.vector.tensor_tensor(out=u[r], in0=u[r], in1=ng, op=ALU.max)
                     mx(MX_LATE)
-                    nc.vector.tensor_scalar_min(out=u[r], in0=u[r], scalar1=0.0)
-                    nc.vector.tensor_tensor(out=u[r], in0=u[r], in1=sgt[:, r, :], op=ALU.mult)
-                    for hh in range(2):
-                        nc.vector.tensor_scalar(
-                            out=humps[:, r, hh, :], in0=u[r], scalar1=(2.0, -2.0)[hh], scalar2=0.0,
-                            op0=ALU.mult, op1=ALU.max,
-                        )
+                    clamp(r)
+                    sign(r)
+                    split(r)
                     quantise(r)
                     stores()
                     for q in made:
@@ -418,7 +399,6 @@ def tile_kanlinearnores_v2_kernel(tc, x, spline_weight, out):
             for step in first[2:]:
                 step()
             x_copy(256, B)
-            late = None
             for ci in range(n_chunks):
                 j, b0, nb, off = chunks[ci]
                 per_step = (SLOTS if ci < FRONT else SLOTS_B) * nb / 256 / 9.0
@@ -438,10 +418,6 @@ def tile_kanlinearnores_v2_kernel(tc, x, spline_weight, out):
                 slots()
                 ahead[0]()
                 outer(0)
-                if late is not None:
-                    late(0)
-                    late(1)
-                    late = None
                 inner()
                 slots()
                 outer(1)
@@ -465,28 +441,24 @@ def tile_kanlinearnores_v2_kernel(tc, x, spline_weight, out):
                     state["open"] = None
                     mx_open(1, 0)
                 slots()
-                clamp()
+                clamp(0)
+                clamp(1)
                 more[2]()
                 ahead[3]()
                 slots()
-                sign()
+                sign(0)
+                sign(1)
                 more[3]()
                 ahead[4]()
                 slots()
                 split(0)
                 ahead[5]()
-                if ci not in S_ACT:
-                    split(1)
+                split(1)
                 more[4]()
                 slots()
-                if ci not in S_ACT:
-                    quantise(0)
+                quantise(0)
                 ahead[6]()
-                if ci in S_ACT:
-                    split(1)
-                    late = quantise
-                else:
-                    quantise(1)
+                quantise(1)
                 more[5]()
                 slots()
                 sg = next_sg

@@ -271,13 +271,12 @@ def tile_kanlinearnores_v2_kernel(tc, x, spline_weight, out):
                 )
 
             def finish():
-                if ci > 0:
-                    made_chunk(ci - 1)
-                for r in range(2):
-                    nc.vector.tensor_tensor(out=u[r], in0=u[r], in1=ng, op=ALU.max)
+                made_chunk(ci - 1)
+                for step in (join, clamp, sign):
+                    step(0)
+                    step(1)
                     mx(MX_LATE)
-                    clamp(r)
-                    sign(r)
+                for r in range(2):
                     split(r)
                     quantise(r)
                     stores()

@@ -383,7 +383,7 @@ def tile_kanlinearnores_v2_kernel(tc, x, spline_weight, out):
             if left[(0, 0)] == left[(1, 0)] == -1 and (2, 1) not in acc:
                 mx_open(1, 1)
 
-        with tc.manual_schedule(engines={mybir.EngineType.PE, mybir.EngineType.Activation, mybir.EngineType.DVE}):
+        with tc.manual_schedule(engines={mybir.EngineType.DVE}):
             w_load(0)
             sg, steps = signs(0)
             mx_open(0, 0)

from contextlib import ExitStack

import concourse.mybir as mybir
from concourse.masks import make_identity

F32 = mybir.dt.float32
BF16 = mybir.dt.bfloat16
U32 = mybir.dt.uint32
U8 = mybir.dt.uint8
FP8X4 = mybir.dt.float8_e4m3fn_x4
ACT = mybir.ActivationFunctionType
ALU = mybir.AluOpType

P = 128
B, IN, OUT, NB = 512, 1024, 1024, 8
K = IN * NB
PASSES = K // 512
FLOPS = 2 * B * K * OUT

SLOTS = 12
FRONT = 4
SLOTS_B = 10
KAPPA = (0, 1, 2, 3)
AHEAD_T = 3
AHEAD_G = 3
MX_SLOT = 12
RUN = 1
MX_LATE = 64
Y_ACT = (8, 9)
R6 = 6.0 ** -0.5


def tile_kanlinearnores_v2_kernel(tc, x, spline_weight, out):
    nc = tc.nc
    w2d = spline_weight.rearrange("o i g -> o (i g)")
    with ExitStack() as ctx:
        keep = ctx.enter_context(tc.tile_pool(name="keep", bufs=1))
        raw = ctx.enter_context(tc.tile_pool(name="raw", bufs=2))
        wgp = ctx.enter_context(tc.tile_pool(name="wgp", bufs=3))
        tmp = ctx.enter_context(tc.tile_pool(name="tmp", bufs=2))
        tm1 = ctx.enter_context(tc.tile_pool(name="tm1", bufs=1))
        sgp = ctx.enter_context(tc.tile_pool(name="sgp", bufs=1))
        utp = ctx.enter_context(tc.tile_pool(name="utp", bufs=1))
        ostp = ctx.enter_context(tc.tile_pool(name="ostp", bufs=4))
        sg2 = ctx.enter_context(tc.tile_pool(name="sg2", bufs=2))
        psum = ctx.enter_context(tc.psum_pool(name="psum", bufs=1))

        ident = keep.tile([P, P], F32)
        wcodes = keep.tile([P, 8, PASSES, P], U32, align_bytes=64)
        wplanes = keep.tile([P, 4, PASSES, P], U8, align_bytes=64)
        bcodes = keep.tile([P, PASSES * B], U32, align_bytes=64)
        bscales = keep.tile([P, PASSES * B], U8, align_bytes=64)
        xt = keep.tile([P, 4 * B * 2], BF16, align_bytes=64)

        xr = raw.tile([P, K], BF16, tag="raw")
        for bt in range(4):
            nc.sync.dma_start(out=xr[:, bt * IN : (bt + 1) * IN], in_=x[bt * P : (bt + 1) * P, :])
        make_identity(nc, ident[:])

        xwords = xr[:, 0 : 4 * IN].bitcast(F32).rearrange("p (t q s) -> p t q s", t=4, s=4)
        xt_words = xt[:].bitcast(F32)
        xt_jb = xt_words.rearrange("p (j b) -> p j b", j=4)
        xbanks = [
            [psum.tile([P, 512], F32, tag="bank%d" % (4 + 2 * jh + bh), name="xbank%d%d" % (jh, bh)) for bh in range(2)]
            for jh in range(2)
        ]
        for bt in range(4):
            for j in range(4):
                col = (j % 2) * 256 + (bt % 2) * P
                nc.tensor.transpose(
                    out=xbanks[j // 2][bt // 2][:, col : col + P], in_=xwords[:, bt, :, j], identity=ident[:]
                )
        def x_copy(b0, b1):
            for jh in range(2):
                dst = xt_jb[:, 2 * jh : 2 * jh + 2, b0:b1]
                src = xbanks[jh][b0 // 256][:].rearrange("p (j b) -> p j b", j=2)[:, :, b0 % 256 : b0 % 256 + b1 - b0]
                if jh == 0:
                    nc.scalar.copy(out=dst, in_=src)
                else:
                    nc.vector.tensor_copy(out=dst, in_=src)

        state = {}
        banks, gathers = {}, {}

        def w_load(t):
            wr = raw.tile([P, K], BF16, tag="raw")
            nc.sync.dma_start(out=wr[:], in_=w2d[t * P : (t + 1) * P, :])
            state["next"] = wr[:].bitcast(F32).rearrange("p (q s) -> p q s", s=32)

        def w_transpose(q):
            t, k = divmod(q, 8)
            if k == 0:
                state["words"] = state["next"]
                if t < 7:
                    w_load(t + 1)
            words = state["words"]
            free = 8 - w_at["first"]
            bank = psum.tile([P, 512], F32, tag="bank%d" % (w_at["first"] + q % free), name="wbank%d" % q)
            for cc in range(2):
                c = 2 * k + cc
                for u in range(2):
                    s = 4 * (2 * (c // 4) + u) + c % 4
                    nc.tensor.transpose(
                        out=bank[:, (2 * cc + u) * P : (2 * cc + u + 1) * P],
                        in_=words[:, :, s],
                        identity=ident[:],
                    )
            banks[q] = bank

        def w_gather(q):
            bank = banks.pop(q)
            if q % 2 == 0:
                gathers[q // 2] = wgp.tile([P, 2048], BF16, align_bytes=64, name="wg")
            wg = gathers[q // 2][:, q % 2 * 1024 : (q % 2 + 1) * 1024]
            nc.scalar.copy(
                out=wg.bitcast(F32).rearrange("p (c o u) -> p c o u", c=2, u=2),
                in_=bank[:].rearrange("p (c u o) -> p c o u", c=2, u=2),
            )

        def w_quantise(q):
            t, k = divmod(q, 4)
            wg = gathers.pop(q)
            nc.vector.quantize_mx(
                out=wcodes[:, t, 4 * k : 4 * k + 4, :].rearrange("p c o -> p (c o)").bitcast(FP8X4),
                scales=wplanes[4 * (t % 2) : P, t // 2, 4 * k : 4 * k + 4, :].rearrange("p c o -> p (c o)"),
                in_=wg[:],
            )

        chunks = []
        for half in range(2):
            for j in range(4):
                sizes = (128, 128) if (half, j) in ((0, 0), (1, 3)) else (256,)
                b0 = 256 * half
                for nb in sizes:
                    chunks.append((j, b0, nb, 4 * (j * B + b0)))
                    b0 += nb
        n_chunks = len(chunks)

        def signs(ci):
            j, b0, nb, off = chunks[ci]
            n = 2 * nb
            xs = xt[:, j * 1024 + 2 * b0 : j * 1024 + 2 * b0 + n]
            ytt = sgp.tile([P, 512, 2], BF16, tag="yt")
            sgtt = sg2.tile([P, 2, 1024], BF16, tag="sgt")
            yt, sgt = ytt[:, 0:n, :], sgtt[:, :, 0 : 2 * n]
            y = yt.rearrange("p n e -> p (n e)")
            return sgt, [
                lambda: nc.scalar.copy(out=yt[:, :, 0], in_=xs)
                if ci in Y_ACT
                else nc.vector.tensor_copy(out=yt[:, :, 0], in_=xs),
                lambda: nc.scalar.activation(out=yt[:, :, 1], in_=xs, func=ACT.Identity, bias=-0.4)
                if ci in Y_ACT
                else nc.vector.tensor_scalar_add(out=yt[:, :, 1], in0=xs, scalar1=-0.4),
                lambda: nc.vector.tensor_scalar(
                    out=sgt[:, 0, :], in0=y, scalar1=-0.6, scalar2=0.5, op0=ALU.is_ge, op1=ALU.subtract
                ),
                lambda: nc.vector.tensor_scalar(
                    out=sgt[:, 1, :], in0=y, scalar1=0.2, scalar2=-1.0 if ci in KAPPA else 1.0, op0=ALU.is_ge, op1=ALU.mult
                ),
                lambda: nc.vector.tensor_scalar(
                    out=y, in0=y, scalar1=-1.402, scalar2=0.5 if ci in KAPPA else -0.5, op0=ALU.is_ge, op1=ALU.mult
                ),
                lambda: nc.vector.tensor_tensor(out=sgt[:, 1, :], in0=sgt[:, 1, :], in1=y, op=ALU.add),
            ]

        def distances(ci):
            j, b0, nb, off = chunks[ci]
            n = 2 * nb
            xs = xt[:, j * 1024 + 2 * b0 : j * 1024 + 2 * b0 + n]
            td = tmp.tile([P, 2, 512], F32, tag="td")
            td2 = tmp.tile([P, 2, 512], F32, tag="td2")
            ta = tm1.tile([P, 2, 512], F32, tag="ta")
            tb = tm1.tile([P, 2, 512], F32, tag="tb")
            th = tm1.tile([P, 2, 512], F32, tag="th")
            tw = tm1.tile([P, 2, 512], F32, tag="tw")
            d0, d2, sa, sb, h, w2 = (t[:, :, 0:n] for t in (td, td2, ta, tb, th, tw))
            state[ci] = (d0, d2, sa, sb, h, w2)

            def first():
                for e in range(2):
                    nc.scalar.activation(out=td[:, e, 0:n], in_=xs, func=ACT.Abs, bias=1.5 - e, scale=2.5)

            if ci in KAPPA:
                r23 = (2.0 / 3.0) ** 0.5
                return [
                    first,
                    lambda: nc.scalar.activation(out=d0, in_=d0, func=ACT.Abs, bias=-2.0, scale=1.0),
                    lambda: nc.scalar.activation(out=d2, in_=d0, func=ACT.Abs, bias=-2.0, scale=1.0),
                    lambda: nc.scalar.activation(out=w2, in_=d2, func=ACT.Square, bias=-r23, scale=r23),
                    lambda: nc.scalar.activation(out=sa, in_=d2, func=ACT.Square, scale=R6),
                    lambda: nc.scalar.activation(out=sb, in_=d2, func=ACT.Square, bias=2.0 * R6, scale=-R6),
                    lambda: None,
                ]
            return [
                first,
                lambda: nc.scalar.activation(out=d0, in_=d0, func=ACT.Abs, bias=-2.0, scale=1.0),
                lambda: nc.scalar.activation(out=d2, in_=d0, func=ACT.Abs, bias=-2.0, scale=1.0),
                lambda: nc.scalar.activation(out=h, in_=d2, func=ACT.Abs, bias=-1.0, scale=1.0),
                lambda: nc.scalar.activation(out=w2, in_=h, func=ACT.Square, bias=1.0, scale=-1.0),
                lambda: nc.scalar.activation(out=sa, in_=d2, func=ACT.Square, scale=R6),
                lambda: nc.scalar.activation(out=sb, in_=d2, func=ACT.Square, bias=2.0 * R6, scale=-R6),
            ]

        def values(ci, sgt):
            j, b0, nb, off = chunks[ci]
            n = 2 * nb
            d0, d2, sa, sb, h, w2 = state.pop(ci)
            ngt = sgp.tile([P, 1, 1024], BF16, tag="ng")
            ut = utp.tile([P, 2, 1024], BF16, tag="ut")
            ob = sgp.tile([P, 4096], BF16, tag="ob", align_bytes=64)
            ng = ngt[:, 0, 0 : 2 * n]
            kap = ci in KAPPA
            u = [ut[:, r, 0 : 2 * n] for r in range(2)]
            humps = ob[:, 0 : 8 * n].rearrange("p (r h n) -> p r h n", r=2, h=2)

            def inner_cubic():
                if kap:
                    nc.vector.scalar_tensor_tensor(out=w2, in0=d2, scalar=1.0, in1=w2, op0=ALU.subtract, op1=ALU.mult)
                    return
                nc.vector.scalar_tensor_tensor(out=w2, in0=h, scalar=1.0, in1=w2, op0=ALU.add, op1=ALU.mult)

            def inner():
                if kap:
                    return
                nc.scalar.activation(
                    out=ng.rearrange("p (n e) -> p n e", e=2), in_=w2.rearrange("p e n -> p n e"),
                    func=ACT.Identity, bias=-2.0 / 3.0, scale=0.5,
                )

            def outer(r):
                dist, sq = ((d0, sa), (d2, sb))[r]
                if kap:
                    nc.vector.scalar_tensor_tensor(out=sq, in0=dist, scalar=2.0, in1=sq, op0=ALU.subtract, op1=ALU.mult)
                    return
                nc.vector.scalar_tensor_tensor(
                    out=u[r].rearrange("p (n e) -> p n e", e=2), in0=dist.rearrange("p e n -> p n e"), scalar=2.0,
                    in1=sq.rearrange("p e n -> p n e"), op0=ALU.subtract, op1=ALU.mult,
                )

            def join(r):
                if kap:
                    nc.vector.scalar_tensor_tensor(
                        out=u[r].rearrange("p (n e) -> p n e", e=2), in0=w2.rearrange("p e n -> p n e"), scalar=0.0,
                        in1=(sa, sb)[r].rearrange("p e n -> p n e"),
                        op0=(ALU.max, ALU.min)[r], op1=(ALU.add, ALU.subtract)[r],
                    )
                else:
                    nc.vector.tensor_tensor(out=u[r], in0=u[r], in1=ng, op=ALU.max)

            def clamp(r):
                if kap and r == 1:
                    nc.vector.tensor_scalar_max(out=u[1], in0=u[1], scalar1=0.0)
                else:
                    nc.vector.tensor_scalar_min(out=u[r], in0=u[r], scalar1=0.0)

            def sign(r):
                nc.vector.tensor_tensor(out=u[r], in0=u[r], in1=sgt[:, r, :], op=ALU.mult)

            def split(r):
                for hh in range(2):
                    nc.vector.tensor_scalar(
                        out=humps[:, r, hh, :], in0=u[r], scalar1=(2.0, -2.0)[hh], scalar2=0.0, op0=ALU.mult, op1=ALU.max
                    )

            def quantise(r):
                w0 = off + r * 2 * nb
                nc.vector.quantize_mx(
                    out=bcodes[:, w0 : w0 + 2 * nb].bitcast(FP8X4),
                    scales=bscales[:, w0 : w0 + 2 * nb],
                    in_=ob[:, r * 4 * n : (r + 1) * 4 * n],
                )

            def finish():
                made_chunk(ci - 1)
                for step in (join, clamp, sign):
                    step(0)
                    step(1)
                    mx(MX_LATE)
                for r in range(2):
                    split(r)
                    quantise(r)
                    stores()
                    for q in made:
                        add(q, ci, (2 * r, 2 * r + 1))
                    mx(1000)
                stores()

            return inner_cubic, inner, outer, join, clamp, sign, split, quantise, finish

        acc, left = {}, {}
        ready = {}
        made = []
        state["chunks_made"] = []

        def mx_pass(t, ci, q, mi):
            j, b0, nb, off = chunks[ci]
            n, tq = divmod(t, 4)
            m = b0 // P + mi
            c = 4 * j + q // 2 + 2 * (q % 2)
            w0 = off + q * nb + mi * P
            nc.tensor.matmul_mx(
                out=acc[(m, n)][:, tq * P : (tq + 1) * P],
                lhsT=bcodes[:, w0 : w0 + P].bitcast(FP8X4),
                lhsT_scale=bscales[:, w0 : w0 + P],
                rhs=wcodes[:, t, c, :].bitcast(FP8X4),
                rhs_scale=wplanes[4 * (t % 2) : P, t // 2, c, :],
                start=left[(m, n)] == 64,
                stop=left[(m, n)] == 1,
            )
            left[(m, n)] -= 1

        def mx(count):
            for key in sorted(ready):
                while key in acc and count > 0 and ready[key]:
                    mx_pass(*ready[key].pop(0))
                    count -= 1

        def mx_open(half, n):
            for m in range(2 * half, 2 * half + 2):
                acc[(m, n)] = psum.tile([P, 512], F32, tag="bank%d" % ((0, 2, 4, 0)[2 * half + n] + m % 2), name="acc%d%d" % (m, n))
                left[(m, n)] = 64
                ready.setdefault((m, n), [])

        def made_unit(q):
            made.append(q)
            for ci in state["chunks_made"]:
                add(q, ci)

        def add(q, ci, rs=(0, 1, 2, 3)):
            t, j = divmod(q, 4)
            if chunks[ci][0] == j:
                for mi in range(chunks[ci][2] // P):
                    todo = ready.setdefault((chunks[ci][1] // P + mi, t // 4), [])
                    todo.extend((t, ci, r, mi) for r in rs)

        def made_chunk(ci):
            state["chunks_made"].append(ci)
            for rs in ((0, 1), (2, 3)):
                for q in made:
                    add(q, ci, rs)

        w_at = {"t": 0, "g": 0, "q": 0, "first": 4, "slot": 0}

        def slot():
            if w_at["q"] == 32:
                mx(MX_LATE)
                return
            w_at["slot"] += 1
            turn = w_at["slot"] % RUN == 0
            if turn or w_at["t"] < RUN:
                for i in range(RUN):
                    if w_at["t"] < 64 and w_at["t"] - w_at["g"] < 8 - w_at["first"]:
                        w_transpose(w_at["t"])
                        w_at["t"] += 1
            if w_at["g"] < 64 and w_at["g"] < w_at["t"] and (w_at["t"] == 64 or w_at["t"] - w_at["g"] >= min(AHEAD_T, 8 - w_at["first"] - RUN + 1)):
                w_gather(w_at["g"])
                w_at["g"] += 1
            if w_at["g"] == 64 or w_at["g"] - 2 * w_at["q"] > AHEAD_G:
                w_quantise(w_at["q"])
                w_at["q"] += 1
                if w_at["q"] > 1:
                    made_unit(w_at["q"] - 2)
                if w_at["q"] == 32:
                    made_unit(31)
            if turn:
                mx(MX_SLOT * RUN)

        def store(m, n, on_act):
            ostt = ostp.tile([P, 512], F32, name="ost")
            ost = ostt[:]
            if on_act:
                nc.scalar.copy(out=ost, in_=acc[(m, n)][:])
            else:
                nc.vector.tensor_copy(out=ost, in_=acc[(m, n)][:])
            nc.sync.dma_start(out=out[m * P : (m + 1) * P, n * 512 : (n + 1) * 512], in_=ost)

        def stores():
            for m in range(4):
                for n in range(2):
                    if left.get((m, n)) == 0:
                        left[(m, n)] = -1
                        store(m, n, m < 3 or n == 0)
            if left[(0, 0)] == left[(1, 0)] == -1 and (2, 1) not in acc:
                mx_open(1, 1)

        with tc.manual_schedule(engines={mybir.EngineType.DVE}):
            w_load(0)
            sg, steps = signs(0)
            mx_open(0, 0)
            mx_open(0, 1)
            x_copy(0, P)
            first = distances(0)
            for step in first[:2]:
                step()
            for step in steps:
                step()
            x_copy(P, 256)
            for step in first[2:]:
                step()
            x_copy(256, B)
            for ci in range(n_chunks):
                j, b0, nb, off = chunks[ci]
                per_step = (SLOTS if ci < FRONT else SLOTS_B) * nb / 256 / 9.0

                def slots():
                    state["due"] = state.get("due", 0.0) + per_step
                    while state["due"] >= 1.0:
                        state["due"] -= 1.0
                        slot()

                ahead, next_sg, more = [lambda: None] * 7, sg, [lambda: None] * 6
                if ci + 1 < n_chunks:
                    ahead = distances(ci + 1)
                    next_sg, more = signs(ci + 1)
                inner_cubic, inner, outer, join, clamp, sign, split, quantise, finish = values(ci, sg)
                inner_cubic()
                slots()
                ahead[0]()
                outer(0)
                inner()
                slots()
                outer(1)
                more[0]()
                ahead[1]()
                slots()
                if ci == n_chunks - 1:
                    finish()
                    break
                join(0)
                more[1]()
                ahead[2]()
                slots()
                join(1)
                if ci > 0:
                    made_chunk(ci - 1)
                    if chunks[ci - 1][1] == 256 and w_at["first"] == 4:
                        w_at["first"] = 6
                        state["open"] = w_at["t"]
                if state.get("open") is not None and w_at["g"] >= state["open"]:
                    state["open"] = None
                    mx_open(1, 0)
                slots()
                clamp(0)
                clamp(1)
                more[2]()
                ahead[3]()
                slots()
                sign(0)
                sign(1)
                more[3]()
                ahead[4]()
                slots()
                split(0)
                ahead[5]()
                split(1)
                more[4]()
                slots()
                quantise(0)
                ahead[6]()
                quantise(1)
                more[5]()
                slots()
                sg = next_sg
                stores()
